import numpy as np
import ml_dtypes


def mxq(x, axis, fmt="e4m3"):
    dtype, down = {"e4m3": (ml_dtypes.float8_e4m3fn, 7), "e5m2": (ml_dtypes.float8_e5m2, 14)}[fmt]
    v = np.moveaxis(np.asarray(x, np.float32).astype(ml_dtypes.bfloat16).astype(np.float64), axis, -1)
    blocks = v.reshape(v.shape[:-1] + (-1, 32))
    amax = np.abs(blocks).max(-1, keepdims=True)
    byte = np.maximum(np.where(amax > 0, np.frexp(amax)[1] - 1 + 127, 0) - down, 1)
    scale = np.exp2(byte - 127.0)
    codes = (blocks / scale).astype(np.float32).astype(dtype).astype(np.float64)
    return np.moveaxis((codes * scale).reshape(v.shape), -1, axis)


WIDE = False


def mx_kscale(k):
    if not WIDE:
        return np.ones(k)
    levels = np.array([10, -10, 5, -5, 0])
    a = np.random.permutation(np.resize(levels, k // 512 * 4)).reshape(k // 512, 4)
    idx = np.arange(k)
    return np.exp2(a[idx // 512, idx % 128 // 32])


BF16 = ml_dtypes.bfloat16


def bf(x):
    return np.asarray(x, np.float32).astype(BF16)


def f64(x):
    return np.asarray(x).astype(np.float64)


T, M, HW, D, DK, H = 16, 512, 768, 1024, 256, 8
EPS = 1e-6
EXTENT = 27.0


def rope_2d(x, pos):
    nt, n, c = x.shape
    half, quarter = c // 2, c // 4
    theta = 100.0 ** (-2.0 * np.arange(quarter) / half)

    def apply(part, p):
        fr = p[..., None] * theta
        cos, sin = np.cos(fr), np.sin(fr)
        pr = part.reshape(nt, n, quarter, 2)
        x1, x2 = pr[..., 0], pr[..., 1]
        return np.stack([x1 * cos - x2 * sin, x1 * sin + x2 * cos], axis=-1).reshape(nt, n, half)

    return np.concatenate([apply(x[:, :, :half], pos[..., 0]), apply(x[:, :, half:], pos[..., 1])], axis=-1)


def layernorm_nobias(x, gamma):
    mu = x.mean(-1, keepdims=True)
    var = ((x - mu) ** 2).mean(-1, keepdims=True)
    return (x - mu) / np.sqrt(var + EPS) * gamma


def setup_inputs():
    s = mx_kscale(D)
    return {"updated_track_tokens": bf(np.random.standard_normal((T, M, D)) * s),
            "tracks": bf(np.random.uniform(0.0, EXTENT, (T, M, 2))),
            "W_k": bf(np.random.standard_normal((DK, D)) / np.sqrt(D) / s),
            "k_gamma": bf(1.0 + 0.1 * np.random.standard_normal(DK))}


def reference(updated_track_tokens, tracks, W_k, k_gamma):
    k = mxq(f64(updated_track_tokens), 2, "e4m3") @ mxq(f64(W_k), 1, "e4m3").T
    k = rope_2d(k, f64(tracks))
    return layernorm_nobias(k, f64(k_gamma))

@@ -1,0 +1,315 @@
+import math
+from contextlib import ExitStack
+
+import concourse.mybir as mybir
+from concourse.masks import make_identity
+
+FP8X4 = mybir.dt.float8_e4m3fn_x4
+BF16 = mybir.dt.bfloat16
+F32 = mybir.dt.float32
+I32 = mybir.dt.int32
+U32 = mybir.dt.uint32
+U8 = mybir.dt.uint8
+ALU = mybir.AluOpType
+ACT = mybir.ActivationFunctionType
+
+P = 128
+TOKENS = 16 * 512
+D_IN = 1024
+D_K = 256
+PAIRS = D_K // 2
+FREQS = PAIRS // 2
+PASSES = 2
+WORDS = D_IN // 2
+TILES = TOKENS // P
+GROUP = 4
+GROUPS = TILES // GROUP
+PLANES = 4
+EPS = 1e-6
+MAGIC = 1.5 * 2.0**23
+ROWS = 16
+BLOCK = P // ROWS
+LOADS_AHEAD = 3
+
+FLOPS = 2 * TOKENS * D_IN * D_K
+
+
+def tile_attentionalsplatting_pa_t_kernel(tc, updated_track_tokens, tracks, W_k, k_gamma, out):
+    nc = tc.nc
+    x_view = updated_track_tokens.rearrange("t (a j) d -> (t a) j d", j=TILES)
+    out_view = out.rearrange("t (a j) c -> (t a) j c", j=TILES)
+    trk_view = tracks.rearrange("t (a j) h -> (t a) (j h)", j=TILES)
+
+    with ExitStack() as ctx:
+        ctx.enter_context(tc.manual_schedule())
+        const = ctx.enter_context(tc.tile_pool(name="const", bufs=1))
+        loads = ctx.enter_context(tc.tile_pool(name="loads", bufs=LOADS_AHEAD + 1))
+        work = ctx.enter_context(tc.tile_pool(name="work", bufs=3))
+        deep = ctx.enter_context(tc.tile_pool(name="deep", bufs=2 * GROUP))
+        ps_t = ctx.enter_context(tc.psum_pool(name="ps_t", bufs=3))
+        ps_k = ctx.enter_context(tc.psum_pool(name="ps_k", bufs=GROUP))
+        ps_f = ctx.enter_context(tc.psum_pool(name="ps_f", bufs=1))
+
+        x_of = {}
+
+        def load(grp):
+            x_sb = loads.tile([P, GROUP * D_IN], BF16)
+            rows = x_view[:, GROUP * grp : GROUP * (grp + 1), :]
+            nc.sync.dma_start(out=x_sb[:], in_=rows.rearrange("p j d -> p (j d)"))
+            x_of[grp] = x_sb
+
+        trk = const.tile([P, 2 * TILES], BF16)
+        nc.sync.dma_start(out=trk[:], in_=trk_view)
+        w_sb = const.tile([P, 2 * D_IN], BF16)
+        nc.sync.dma_start(out=w_sb[:], in_=W_k.rearrange("(m e) k -> m (e k)", e=2))
+        for grp in range(LOADS_AHEAD):
+            load(grp)
+
+        ident_f = const.tile([P, P], F32)
+        make_identity(nc, ident_f[:])
+        idx_i = const.tile([P, 1], I32)
+        for h in range(2):
+            nc.gpsimd.iota(idx_i[FREQS * h : FREQS * (h + 1), :], pattern=[[1, 1]], base=0, channel_multiplier=1)
+        hundred = const.tile([P, 1], F32)
+        nc.gpsimd.memset(hundred[:], 100.0)
+        expo = const.tile([P, 1], F32)
+        nc.vector.tensor_scalar(
+            out=expo[:], in0=idx_i[:], scalar1=-1.0 / FREQS, scalar2=-math.log(2.0 * math.pi) / math.log(100.0),
+            op0=ALU.mult, op1=ALU.add,
+        )
+        turns = const.tile([P, 1], F32)
+        nc.gpsimd.tensor_tensor(out=turns[:], in0=hundred[:], in1=expo[:], op=ALU.pow)
+        ident_b = const.tile([P, P], BF16)
+        make_identity(nc, ident_b[:])
+        neg_half = const.tile([P, GROUP], F32)
+        nc.gpsimd.memset(neg_half[:], -0.5)
+        gamma_bf = const.tile([P, D_K], BF16)
+        nc.gpsimd.dma_start(out=gamma_bf[:], in_=k_gamma.partition_broadcast(P))
+
+        pieces = const.tile([P, 3], BF16)
+        rest1 = const.tile([P, 1], F32)
+        rest2 = const.tile([P, 1], F32)
+        nc.vector.tensor_copy(out=pieces[:, 0:1], in_=turns[:])
+        nc.vector.tensor_tensor(out=rest1[:], in0=turns[:], in1=pieces[:, 0:1], op=ALU.subtract)
+        nc.vector.tensor_copy(out=pieces[:, 1:2], in_=rest1[:])
+        nc.vector.tensor_tensor(out=rest2[:], in0=rest1[:], in1=pieces[:, 1:2], op=ALU.subtract)
+        nc.vector.tensor_copy(out=pieces[:, 2:3], in_=rest2[:])
+        coef = const.tile([P, ROWS // 2], BF16)
+        nc.vector.memset(coef[:], 0.0)
+        nc.vector.memset(coef[:, 6:8], MAGIC)
+        for h in range(2):
+            nc.vector.tensor_copy(out=coef[FREQS * h : FREQS * (h + 1), 3 * h : 3 * h + 3], in_=pieces[FREQS * h : FREQS * (h + 1), :])
+        big_t = const.tile([P, BLOCK, P], BF16)
+        nc.vector.memset(big_t[:], 0.0)
+        for a in range(BLOCK):
+            nc.vector.tensor_copy(
+                out=big_t[:, a, ROWS * a : ROWS * (a + 1)].rearrange("m (s r) -> m s r", s=2),
+                in_=coef[:].unsqueeze(1).to_broadcast([P, 2, ROWS // 2]),
+            )
+        big_ps = ps_k.tile([P, BLOCK, P], BF16, tag="kk")
+        for a in range(BLOCK):
+            nc.tensor.transpose(out=big_ps[:, a, :], in_=big_t[:, a, :], identity=ident_b[:])
+        big = const.tile([P, BLOCK, P], BF16)
+        nc.vector.tensor_copy(out=big[:], in_=big_ps[:])
+
+        pos = const.tile([P, TILES, ROWS], BF16)
+        trk_rep = trk[:].rearrange("p (j h) -> p j h", h=2).unsqueeze(3).to_broadcast([P, TILES, 2, 3])
+        nc.vector.memset(pos[:], 0.0)
+        nc.vector.memset(pos[:, :, 6:7], 1.0)
+        nc.vector.memset(pos[:, :, 7:8], -1.0)
+        nc.vector.tensor_copy(out=pos[:, :, 0:6].rearrange("p j (h s) -> p j h s", h=2), in_=trk_rep)
+        nc.vector.tensor_scalar(
+            out=pos[:, :, 8:14].rearrange("p j (h s) -> p j h s", h=2), in0=trk_rep, scalar1=-1.0, scalar2=None, op0=ALU.mult
+        )
+        pos_ps = ps_k.tile([P, TILES // BLOCK, P], BF16, tag="kk")
+        for b in range(TILES // BLOCK):
+            nc.tensor.transpose(
+                out=pos_ps[:, b, :],
+                in_=pos[:, BLOCK * b : BLOCK * (b + 1), :].rearrange("p j r -> p (j r)"),
+                identity=ident_b[:],
+            )
+        pos_t = const.tile([P, TILES // BLOCK, P], BF16)
+        nc.vector.tensor_copy(out=pos_t[:], in_=pos_ps[:])
+        zero = const.tile([P, 1], F32)
+        nc.vector.memset(zero[:], 0.0)
+        half_pi = const.tile([P, 1], F32)
+        nc.vector.tensor_scalar(out=half_pi[:], in0=zero[:], scalar1=math.pi / 2.0, scalar2=None, op0=ALU.add)
+
+        w_neg = const.tile([P, D_IN], BF16)
+        nc.vector.tensor_scalar(out=w_neg[:], in0=w_sb[:, D_IN : 2 * D_IN], scalar1=-1.0, scalar2=None, op0=ALU.mult)
+        w_grouped = const.tile([P, PASSES * PLANES * P * 4], BF16, align_bytes=64)
+        w_grouped5 = w_grouped[:].bitcast(F32).rearrange("q (g l m u) -> q g l m u", g=PASSES, l=PLANES, u=2)
+        w_codes = const.tile([P, PASSES, PLANES * P], U32, align_bytes=64)
+        w_scales = const.tile([P, PASSES, PLANES * P], U8, align_bytes=64)
+        sources = ((w_sb[:, 0:D_IN], (0, 3)), (w_neg[:], (1,)), (w_sb[:, D_IN : 2 * D_IN], (2,)))
+        for rows, fills in sources:
+            wt = ps_t.tile([P, 4, P], F32, tag="t")
+            for s in range(4):
+                nc.tensor.transpose(out=wt[:, s, :], in_=rows.bitcast(F32)[:, P * s : P * (s + 1)], identity=ident_f[:])
+            for l in fills:
+                nc.vector.tensor_copy(out=w_grouped5[:, :, l, :, :], in_=wt[:].rearrange("q (g u) m -> q g m u", u=2))
+        for g in range(PASSES):
+            nc.vector.quantize_mx(
+                out=w_codes[:, g, :].bitcast(FP8X4),
+                scales=w_scales[:, g, :],
+                in_=w_grouped[:, 2048 * g : 2048 * (g + 1)],
+            )
+        gamma = const.tile([P, D_K], F32)
+        nc.vector.tensor_copy(out=gamma[:], in_=gamma_bf[:])
+
+        grouped_of = {}
+        codes_of = {}
+        table_of = {}
+        kk_of = {}
+        prod_of = {}
+        cent_of = {}
+        mean_of = {}
+        rstd_of = {}
+
+        def transpose_tile(grp, j):
+            if j == 0:
+                x_grouped = work.tile([P, GROUP * D_IN], BF16, align_bytes=64)
+                grouped_of[grp] = x_grouped
+            x32 = x_of[grp][:].bitcast(F32)
+            xt = ps_t.tile([P, 4, P], F32, tag="t")
+            for s in range(4):
+                first = WORDS * j + P * s
+                nc.tensor.transpose(out=xt[:, s, :], in_=x32[:, first : first + P], identity=ident_f[:])
+            nc.scalar.copy(
+                out=grouped_of[grp][:].bitcast(F32)[:, WORDS * j : WORDS * (j + 1)].rearrange("q (g t u) -> q g t u", g=PASSES, u=2),
+                in_=xt[:].rearrange("q (g u) t -> q g t u", u=2),
+            )
+
+        def quantise(grp):
+            x_codes = work.tile([P, GROUP * PASSES * P], U32, align_bytes=64)
+            x_scales = work.tile([P, GROUP * PASSES * P], U8, align_bytes=64)
+            for c in range(2):
+                nc.vector.quantize_mx(
+                    out=x_codes[:, 512 * c : 512 * (c + 1)].bitcast(FP8X4),
+                    scales=x_scales[:, 512 * c : 512 * (c + 1)],
+                    in_=grouped_of[grp][:, 2048 * c : 2048 * (c + 1)],
+                )
+            codes_of[grp] = (x_codes, x_scales)
+
+        def angles(grp):
+            frac = ps_f.tile([P, GROUP * PAIRS], F32)
+            a0 = (GROUP * grp) % BLOCK
+            nc.tensor.matmul(
+                out=frac[:],
+                lhsT=pos_t[:, (GROUP * grp) // BLOCK, :],
+                rhs=big[:, a0 : a0 + GROUP, :].rearrange("k a m -> k (a m)"),
+                start=True,
+                stop=True,
+            )
+            table = work.tile([P, GROUP * 2 * PAIRS], F32)
+            table4 = table[:].rearrange("p (j r m) -> p j r m", j=GROUP, r=2)
+            nc.scalar.activation(
+                out=table4[:, :, 1, :], in_=frac[:].rearrange("p (j m) -> p j m", j=GROUP), func=ACT.Sin, scale=-2.0 * math.pi
+            )
+            frac_abs = work.tile([P, GROUP * PAIRS], F32)
+            nc.scalar.activation(out=frac_abs[:], in_=frac[:], func=ACT.Abs)
+            nc.scalar.activation(
+                out=table4[:, :, 0, :],
+                in_=frac_abs[:].rearrange("p (j m) -> p j m", j=GROUP),
+                func=ACT.Sin,
+                scale=-2.0 * math.pi,
+                bias=half_pi[:],
+            )
+            table_of[grp] = table
+
+        def project_tile(grp, j):
+            x_codes, x_scales = codes_of[grp]
+            kk = ps_k.tile([P, PLANES * P], F32, tag="kk")
+            for g in range(PASSES):
+                first = (PASSES * j + g) * P
+                nc.tensor.matmul_mx(
+                    out=kk[:],
+                    lhsT=x_codes[:, first : first + P].bitcast(FP8X4),
+                    lhsT_scale=x_scales[:, first : first + P],
+                    rhs=w_codes[:, g, :].bitcast(FP8X4),
+                    rhs_scale=w_scales[:, g, :],
+                    start=(g == 0),
+                    stop=(g == PASSES - 1),
+                )
+            kk_of[(grp, j)] = kk
+
+        def rotate(grp):
+            sum_r = work.tile([P, GROUP], F32)
+            for j in range(GROUP):
+                prod = deep.tile([P, PLANES * P], F32)
+                nc.vector.scalar_tensor_tensor(
+                    out=prod[:].rearrange("p (d x) -> p d x", d=2),
+                    in0=kk_of[(grp, j)][:].rearrange("p (d x) -> p d x", d=2),
+                    scalar=1.0,
+                    in1=table_of[grp][:, D_K * j : D_K * (j + 1)].unsqueeze(1).to_broadcast([P, 2, D_K]),
+                    op0=ALU.mult,
+                    op1=ALU.mult,
+                    accum_out=sum_r[:, j : j + 1],
+                )
+                prod_of[(grp, j)] = prod
+            mean = work.tile([P, GROUP], F32)
+            nc.vector.tensor_scalar(out=mean[:], in0=sum_r[:], scalar1=1.0 / D_K, scalar2=None, op0=ALU.mult)
+            mean_of[grp] = mean
+
+        def centre(grp):
+            for j in range(GROUP):
+                prod4 = prod_of[(grp, j)][:].rearrange("p (e t m) -> p e t m", e=2, t=2)
+                cent = deep.tile([P, D_K], F32)
+                nc.vector.scalar_tensor_tensor(
+                    out=cent[:].rearrange("p (e m) -> p e m", e=2),
+                    in0=prod4[:, :, 0, :],
+                    scalar=mean_of[grp][:, j : j + 1],
+                    in1=prod4[:, :, 1, :],
+                    op0=ALU.subtract,
+                    op1=ALU.add,
+                )
+                cent_of[(grp, j)] = cent
+
+        def deviation(grp):
+            sum_sq = work.tile([P, GROUP], F32)
+            for j in range(GROUP):
+                squares = deep.tile([P, D_K], F32)
+                nc.scalar.activation(out=squares[:], in_=cent_of[(grp, j)][:], func=ACT.Square, accum_out=sum_sq[:, j : j + 1])
+            var = work.tile([P, GROUP], F32)
+            nc.gpsimd.tensor_scalar(out=var[:], in0=sum_sq[:], scalar1=1.0 / D_K, scalar2=EPS, op0=ALU.mult, op1=ALU.add)
+            rstd = work.tile([P, GROUP], F32)
+            nc.gpsimd.tensor_tensor(out=rstd[:], in0=var[:], in1=neg_half[:], op=ALU.pow)
+            rstd_of[grp] = rstd
+
+        def scale_and_store(grp):
+            o_sb = work.tile([P, GROUP * D_K], F32)
+            for j in range(GROUP):
+                nc.vector.scalar_tensor_tensor(
+                    out=o_sb[:, D_K * j : D_K * (j + 1)].rearrange("p (m e) -> p m e", e=2),
+                    in0=cent_of[(grp, j)][:].rearrange("p (e m) -> p m e", e=2),
+                    scalar=rstd_of[grp][:, j : j + 1],
+                    in1=gamma[:].rearrange("p (m e) -> p m e", e=2),
+                    op0=ALU.mult,
+                    op1=ALU.mult,
+                )
+            rows = out_view[:, GROUP * grp : GROUP * (grp + 1), :]
+            nc.sync.dma_start(out=rows.rearrange("p j c -> p (j c)"), in_=o_sb[:])
+
+        def live(grp):
+            return 0 <= grp < GROUPS
+
+        for i in range(-2, GROUPS + 1):
+            if live(i + LOADS_AHEAD) and i + LOADS_AHEAD >= LOADS_AHEAD:
+                load(i + LOADS_AHEAD)
+            if live(i + 1):
+                quantise(i + 1)
+            if live(i - 1):
+                deviation(i - 1)
+            if live(i + 1):
+                angles(i + 1)
+            if live(i):
+                rotate(i)
+            for j in range(GROUP):
+                if live(i + 2):
+                    transpose_tile(i + 2, j)
+                if live(i + 1):
+                    project_tile(i + 1, j)
+            if live(i):
+                centre(i)
+            if live(i - 1):
+                scale_and_store(i - 1)

@@ -54,8 +54,12 @@ def tile_attentionalsplatting_pa_t_kernel(tc, updated_track_tokens, tracks, W_k,
 
         def load(grp):
             x_sb = loads.tile([P, GROUP * D_IN], BF16)
-            rows = x_view[:, GROUP * grp : GROUP * (grp + 1), :]
-            nc.sync.dma_start(out=x_sb[:], in_=rows.rearrange("p j d -> p (j d)"))
+            for c in range(2):
+                first = GROUP * grp + 2 * c
+                nc.sync.dma_start(
+                    out=x_sb[:, 2 * D_IN * c : 2 * D_IN * (c + 1)],
+                    in_=x_view[:, first : first + 2, :].rearrange("p j d -> p (j d)"),
+                )
             x_of[grp] = x_sb
 
         trk = const.tile([P, 2 * TILES], BF16)
@@ -66,7 +70,23 @@ def tile_attentionalsplatting_pa_t_kernel(tc, updated_track_tokens, tracks, W_k,
             load(grp)
 
         ident_f = const.tile([P, P], F32)
-        make_identity(nc, ident_f[:])
+        nc.vector.memset(ident_f[:], 0.0)
+        make_identity(nc, ident_f[:], nomemset=True)
+        ident_b = const.tile([P, P], BF16)
+        nc.vector.memset(ident_b[:], 0.0)
+        coef = const.tile([P, ROWS // 2], BF16)
+        nc.vector.memset(coef[:], 0.0)
+        nc.vector.memset(coef[:, 6:8], MAGIC)
+        big_t = const.tile([P, BLOCK, P], BF16)
+        nc.vector.memset(big_t[:], 0.0)
+        pos = const.tile([P, TILES, ROWS], BF16)
+        nc.vector.memset(pos[:], 0.0)
+        nc.vector.memset(pos[:, :, 6:7], 1.0)
+        nc.vector.memset(pos[:, :, 7:8], -1.0)
+        zero = const.tile([P, 1], F32)
+        nc.vector.memset(zero[:], 0.0)
+        half_pi = const.tile([P, 1], F32)
+        nc.vector.tensor_scalar(out=half_pi[:], in0=zero[:], scalar1=math.pi / 2.0, scalar2=None, op0=ALU.add)
         idx_i = const.tile([P, 1], I32)
         for h in range(2):
             nc.gpsimd.iota(idx_i[FREQS * h : FREQS * (h + 1), :], pattern=[[1, 1]], base=0, channel_multiplier=1)
@@ -79,8 +99,7 @@ def tile_attentionalsplatting_pa_t_kernel(tc, updated_track_tokens, tracks, W_k,
         )
         turns = const.tile([P, 1], F32)
         nc.gpsimd.tensor_tensor(out=turns[:], in0=hundred[:], in1=expo[:], op=ALU.pow)
-        ident_b = const.tile([P, P], BF16)
-        make_identity(nc, ident_b[:])
+        make_identity(nc, ident_b[:], nomemset=True)
         neg_half = const.tile([P, GROUP], F32)
         nc.gpsimd.memset(neg_half[:], -0.5)
         gamma_bf = const.tile([P, D_K], BF16)
@@ -94,46 +113,19 @@ def tile_attentionalsplatting_pa_t_kernel(tc, updated_track_tokens, tracks, W_k,
         nc.vector.tensor_copy(out=pieces[:, 1:2], in_=rest1[:])
         nc.vector.tensor_tensor(out=rest2[:], in0=rest1[:], in1=pieces[:, 1:2], op=ALU.subtract)
         nc.vector.tensor_copy(out=pieces[:, 2:3], in_=rest2[:])
-        coef = const.tile([P, ROWS // 2], BF16)
-        nc.vector.memset(coef[:], 0.0)
-        nc.vector.memset(coef[:, 6:8], MAGIC)
         for h in range(2):
             nc.vector.tensor_copy(out=coef[FREQS * h : FREQS * (h + 1), 3 * h : 3 * h + 3], in_=pieces[FREQS * h : FREQS * (h + 1), :])
-        big_t = const.tile([P, BLOCK, P], BF16)
-        nc.vector.memset(big_t[:], 0.0)
         for a in range(BLOCK):
             nc.vector.tensor_copy(
                 out=big_t[:, a, ROWS * a : ROWS * (a + 1)].rearrange("m (s r) -> m s r", s=2),
                 in_=coef[:].unsqueeze(1).to_broadcast([P, 2, ROWS // 2]),
             )
-        big_ps = ps_k.tile([P, BLOCK, P], BF16, tag="kk")
-        for a in range(BLOCK):
-            nc.tensor.transpose(out=big_ps[:, a, :], in_=big_t[:, a, :], identity=ident_b[:])
-        big = const.tile([P, BLOCK, P], BF16)
-        nc.vector.tensor_copy(out=big[:], in_=big_ps[:])
 
-        pos = const.tile([P, TILES, ROWS], BF16)
         trk_rep = trk[:].rearrange("p (j h) -> p j h", h=2).unsqueeze(3).to_broadcast([P, TILES, 2, 3])
-        nc.vector.memset(pos[:], 0.0)
-        nc.vector.memset(pos[:, :, 6:7], 1.0)
-        nc.vector.memset(pos[:, :, 7:8], -1.0)
         nc.vector.tensor_copy(out=pos[:, :, 0:6].rearrange("p j (h s) -> p j h s", h=2), in_=trk_rep)
         nc.vector.tensor_scalar(
             out=pos[:, :, 8:14].rearrange("p j (h s) -> p j h s", h=2), in0=trk_rep, scalar1=-1.0, scalar2=None, op0=ALU.mult
         )
-        pos_ps = ps_k.tile([P, TILES // BLOCK, P], BF16, tag="kk")
-        for b in range(TILES // BLOCK):
-            nc.tensor.transpose(
-                out=pos_ps[:, b, :],
-                in_=pos[:, BLOCK * b : BLOCK * (b + 1), :].rearrange("p j r -> p (j r)"),
-                identity=ident_b[:],
-            )
-        pos_t = const.tile([P, TILES // BLOCK, P], BF16)
-        nc.vector.tensor_copy(out=pos_t[:], in_=pos_ps[:])
-        zero = const.tile([P, 1], F32)
-        nc.vector.memset(zero[:], 0.0)
-        half_pi = const.tile([P, 1], F32)
-        nc.vector.tensor_scalar(out=half_pi[:], in0=zero[:], scalar1=math.pi / 2.0, scalar2=None, op0=ALU.add)
 
         w_neg = const.tile([P, D_IN], BF16)
         nc.vector.tensor_scalar(out=w_neg[:], in0=w_sb[:, D_IN : 2 * D_IN], scalar1=-1.0, scalar2=None, op0=ALU.mult)
@@ -154,8 +146,6 @@ def tile_attentionalsplatting_pa_t_kernel(tc, updated_track_tokens, tracks, W_k,
                 scales=w_scales[:, g, :],
                 in_=w_grouped[:, 2048 * g : 2048 * (g + 1)],
             )
-        gamma = const.tile([P, D_K], F32)
-        nc.vector.tensor_copy(out=gamma[:], in_=gamma_bf[:])
 
         grouped_of = {}
         codes_of = {}
@@ -283,7 +273,7 @@ def tile_attentionalsplatting_pa_t_kernel(tc, updated_track_tokens, tracks, W_k,
                     out=o_sb[:, D_K * j : D_K * (j + 1)].rearrange("p (m e) -> p m e", e=2),
                     in0=cent_of[(grp, j)][:].rearrange("p (e m) -> p m e", e=2),
                     scalar=rstd_of[grp][:, j : j + 1],
-                    in1=gamma[:].rearrange("p (m e) -> p m e", e=2),
+                    in1=gamma_bf[:].rearrange("p (m e) -> p m e", e=2),
                     op0=ALU.mult,
                     op1=ALU.mult,
                 )
@@ -293,23 +283,44 @@ def tile_attentionalsplatting_pa_t_kernel(tc, updated_track_tokens, tracks, W_k,
         def live(grp):
             return 0 <= grp < GROUPS
 
-        for i in range(-2, GROUPS + 1):
-            if live(i + LOADS_AHEAD) and i + LOADS_AHEAD >= LOADS_AHEAD:
+        for j in range(GROUP):
+            transpose_tile(0, j)
+        big_ps = ps_k.tile([P, BLOCK, P], BF16, tag="kk")
+        for a in range(BLOCK):
+            nc.tensor.transpose(out=big_ps[:, a, :], in_=big_t[:, a, :], identity=ident_b[:])
+        big = const.tile([P, BLOCK, P], BF16)
+        nc.vector.tensor_copy(out=big[:], in_=big_ps[:])
+        pos_ps = ps_k.tile([P, TILES // BLOCK, P], BF16, tag="kk")
+        for b in range(TILES // BLOCK):
+            nc.tensor.transpose(
+                out=pos_ps[:, b, :],
+                in_=pos[:, BLOCK * b : BLOCK * (b + 1), :].rearrange("p j r -> p (j r)"),
+                identity=ident_b[:],
+            )
+        pos_t = const.tile([P, TILES // BLOCK, P], BF16)
+        nc.vector.tensor_copy(out=pos_t[:], in_=pos_ps[:])
+        angles(0)
+        quantise(0)
+        for j in range(GROUP):
+            project_tile(0, j)
+        for j in range(GROUP):
+            transpose_tile(1, j)
+        for i in range(GROUPS + 1):
+            if live(i + LOADS_AHEAD):
                 load(i + LOADS_AHEAD)
             if live(i + 1):
-                quantise(i + 1)
-            if live(i - 1):
-                deviation(i - 1)
-            if live(i + 1):
                 angles(i + 1)
+            if live(i + 2):
+                for j in range(GROUP):
+                    transpose_tile(i + 2, j)
             if live(i):
                 rotate(i)
-            for j in range(GROUP):
-                if live(i + 2):
-                    transpose_tile(i + 2, j)
-                if live(i + 1):
+            if live(i + 1):
+                quantise(i + 1)
+                for j in range(GROUP):
                     project_tile(i + 1, j)
             if live(i):
                 centre(i)
+                deviation(i)
             if live(i - 1):
                 scale_and_store(i - 1)

@@ -29,7 +29,12 @@ EPS = 1e-6
 MAGIC = 1.5 * 2.0**23
 ROWS = 16
 BLOCK = P // ROWS
-LOADS_AHEAD = 3
+LOADS_AHEAD = 4
+AHEAD_TRANSPOSE = 6
+AHEAD_QUANTISE = 5
+AHEAD_PROJECT = 4
+BEHIND_CENTRE = 4
+BEHIND_SCALE = 10
 
 FLOPS = 2 * TOKENS * D_IN * D_K
 
@@ -149,39 +154,37 @@ def tile_attentionalsplatting_pa_t_kernel(tc, updated_track_tokens, tracks, W_k,
 
         grouped_of = {}
         codes_of = {}
+        frac_of = {}
         table_of = {}
         kk_of = {}
         prod_of = {}
         cent_of = {}
+        sum_of = {}
         mean_of = {}
+        square_of = {}
         rstd_of = {}
+        o_of = {}
 
-        def transpose_tile(grp, j):
-            if j == 0:
-                x_grouped = work.tile([P, GROUP * D_IN], BF16, align_bytes=64)
-                grouped_of[grp] = x_grouped
-            x32 = x_of[grp][:].bitcast(F32)
+        def transpose_tile(n):
+            first = WORDS * (n % GROUP)
+            x32 = x_of[n // GROUP][:].bitcast(F32)
             xt = ps_t.tile([P, 4, P], F32, tag="t")
-            for s in range(4):
-                first = WORDS * j + P * s
-                nc.tensor.transpose(out=xt[:, s, :], in_=x32[:, first : first + P], identity=ident_f[:])
+            for s4 in range(4):
+                nc.tensor.transpose(out=xt[:, s4, :], in_=x32[:, first + P * s4 : first + P * (s4 + 1)], identity=ident_f[:])
+            x_grouped = work.tile([P, D_IN], BF16, align_bytes=64)
             nc.scalar.copy(
-                out=grouped_of[grp][:].bitcast(F32)[:, WORDS * j : WORDS * (j + 1)].rearrange("q (g t u) -> q g t u", g=PASSES, u=2),
+                out=x_grouped[:].bitcast(F32).rearrange("q (g t u) -> q g t u", g=PASSES, u=2),
                 in_=xt[:].rearrange("q (g u) t -> q g t u", u=2),
             )
+            grouped_of[n] = x_grouped
 
-        def quantise(grp):
-            x_codes = work.tile([P, GROUP * PASSES * P], U32, align_bytes=64)
-            x_scales = work.tile([P, GROUP * PASSES * P], U8, align_bytes=64)
-            for c in range(2):
-                nc.vector.quantize_mx(
-                    out=x_codes[:, 512 * c : 512 * (c + 1)].bitcast(FP8X4),
-                    scales=x_scales[:, 512 * c : 512 * (c + 1)],
-                    in_=grouped_of[grp][:, 2048 * c : 2048 * (c + 1)],
-                )
-            codes_of[grp] = (x_codes, x_scales)
+        def quantise(n):
+            x_codes = work.tile([P, PASSES * P], U32, align_bytes=64)
+            x_scales = work.tile([P, PASSES * P], U8, align_bytes=64)
+            nc.vector.quantize_mx(out=x_codes[:].bitcast(FP8X4), scales=x_scales[:], in_=grouped_of[n][:])
+            codes_of[n] = (x_codes, x_scales)
 
-        def angles(grp):
+        def angle_matmul(grp):
             frac = ps_f.tile([P, GROUP * PAIRS], F32)
             a0 = (GROUP * grp) % BLOCK
             nc.tensor.matmul(
@@ -191,100 +194,113 @@ def tile_attentionalsplatting_pa_t_kernel(tc, updated_track_tokens, tracks, W_k,
                 start=True,
                 stop=True,
             )
-            table = work.tile([P, GROUP * 2 * PAIRS], F32)
-            table4 = table[:].rearrange("p (j r m) -> p j r m", j=GROUP, r=2)
-            nc.scalar.activation(
-                out=table4[:, :, 1, :], in_=frac[:].rearrange("p (j m) -> p j m", j=GROUP), func=ACT.Sin, scale=-2.0 * math.pi
-            )
             frac_abs = work.tile([P, GROUP * PAIRS], F32)
-            nc.scalar.activation(out=frac_abs[:], in_=frac[:], func=ACT.Abs)
-            nc.scalar.activation(
-                out=table4[:, :, 0, :],
-                in_=frac_abs[:].rearrange("p (j m) -> p j m", j=GROUP),
-                func=ACT.Sin,
-                scale=-2.0 * math.pi,
-                bias=half_pi[:],
-            )
+            table = work.tile([P, GROUP * 2 * PAIRS], F32)
+            frac_of[grp] = (frac, frac_abs)
             table_of[grp] = table
 
-        def project_tile(grp, j):
-            x_codes, x_scales = codes_of[grp]
+        def sine_step(grp, step):
+            frac, frac_abs = frac_of[grp]
+            table4 = table_of[grp][:].rearrange("p (j r m) -> p j r m", j=GROUP, r=2)
+            if step == 0:
+                nc.scalar.activation(out=frac_abs[:], in_=frac[:], func=ACT.Abs)
+            elif step == 1:
+                nc.scalar.activation(
+                    out=table4[:, :, 1, :], in_=frac[:].rearrange("p (j m) -> p j m", j=GROUP), func=ACT.Sin, scale=-2.0 * math.pi
+                )
+            else:
+                nc.scalar.activation(
+                    out=table4[:, :, 0, :],
+                    in_=frac_abs[:].rearrange("p (j m) -> p j m", j=GROUP),
+                    func=ACT.Sin,
+                    scale=-2.0 * math.pi,
+                    bias=half_pi[:],
+                )
+
+        def project(n):
+            x_codes, x_scales = codes_of[n]
             kk = ps_k.tile([P, PLANES * P], F32, tag="kk")
             for g in range(PASSES):
-                first = (PASSES * j + g) * P
                 nc.tensor.matmul_mx(
                     out=kk[:],
-                    lhsT=x_codes[:, first : first + P].bitcast(FP8X4),
-                    lhsT_scale=x_scales[:, first : first + P],
+                    lhsT=x_codes[:, P * g : P * (g + 1)].bitcast(FP8X4),
+                    lhsT_scale=x_scales[:, P * g : P * (g + 1)],
                     rhs=w_codes[:, g, :].bitcast(FP8X4),
                     rhs_scale=w_scales[:, g, :],
                     start=(g == 0),
                     stop=(g == PASSES - 1),
                 )
-            kk_of[(grp, j)] = kk
+            kk_of[n] = kk
 
-        def rotate(grp):
-            sum_r = work.tile([P, GROUP], F32)
-            for j in range(GROUP):
-                prod = deep.tile([P, PLANES * P], F32)
-                nc.vector.scalar_tensor_tensor(
-                    out=prod[:].rearrange("p (d x) -> p d x", d=2),
-                    in0=kk_of[(grp, j)][:].rearrange("p (d x) -> p d x", d=2),
-                    scalar=1.0,
-                    in1=table_of[grp][:, D_K * j : D_K * (j + 1)].unsqueeze(1).to_broadcast([P, 2, D_K]),
-                    op0=ALU.mult,
-                    op1=ALU.mult,
-                    accum_out=sum_r[:, j : j + 1],
-                )
-                prod_of[(grp, j)] = prod
+        def rotate(n):
+            grp, j = n // GROUP, n % GROUP
+            if j == 0:
+                sum_r = work.tile([P, GROUP], F32)
+                sum_of[grp] = sum_r
+            prod = deep.tile([P, PLANES * P], F32)
+            nc.vector.scalar_tensor_tensor(
+                out=prod[:].rearrange("p (d x) -> p d x", d=2),
+                in0=kk_of[n][:].rearrange("p (d x) -> p d x", d=2),
+                scalar=1.0,
+                in1=table_of[grp][:, D_K * j : D_K * (j + 1)].unsqueeze(1).to_broadcast([P, 2, D_K]),
+                op0=ALU.mult,
+                op1=ALU.mult,
+                accum_out=sum_of[grp][:, j : j + 1],
+            )
+            prod_of[n] = prod
+
+        def take_mean(grp):
             mean = work.tile([P, GROUP], F32)
-            nc.vector.tensor_scalar(out=mean[:], in0=sum_r[:], scalar1=1.0 / D_K, scalar2=None, op0=ALU.mult)
+            nc.vector.tensor_scalar(out=mean[:], in0=sum_of[grp][:], scalar1=1.0 / D_K, scalar2=None, op0=ALU.mult)
             mean_of[grp] = mean
 
-        def centre(grp):
-            for j in range(GROUP):
-                prod4 = prod_of[(grp, j)][:].rearrange("p (e t m) -> p e t m", e=2, t=2)
-                cent = deep.tile([P, D_K], F32)
-                nc.vector.scalar_tensor_tensor(
-                    out=cent[:].rearrange("p (e m) -> p e m", e=2),
-                    in0=prod4[:, :, 0, :],
-                    scalar=mean_of[grp][:, j : j + 1],
-                    in1=prod4[:, :, 1, :],
-                    op0=ALU.subtract,
-                    op1=ALU.add,
-                )
-                cent_of[(grp, j)] = cent
+        def centre(n):
+            grp, j = n // GROUP, n % GROUP
+            prod4 = prod_of[n][:].rearrange("p (e t m) -> p e t m", e=2, t=2)
+            cent = deep.tile([P, D_K], F32)
+            nc.vector.scalar_tensor_tensor(
+                out=cent[:].rearrange("p (e m) -> p e m", e=2),
+                in0=prod4[:, :, 0, :],
+                scalar=mean_of[grp][:, j : j + 1],
+                in1=prod4[:, :, 1, :],
+                op0=ALU.subtract,
+                op1=ALU.add,
+            )
+            cent_of[n] = cent
+            if j == 0:
+                sum_sq = work.tile([P, GROUP], F32)
+                square_of[grp] = sum_sq
+            squares = deep.tile([P, D_K], F32)
+            nc.scalar.activation(out=squares[:], in_=cent[:], func=ACT.Square, accum_out=square_of[grp][:, j : j + 1])
 
-        def deviation(grp):
-            sum_sq = work.tile([P, GROUP], F32)
-            for j in range(GROUP):
-                squares = deep.tile([P, D_K], F32)
-                nc.scalar.activation(out=squares[:], in_=cent_of[(grp, j)][:], func=ACT.Square, accum_out=sum_sq[:, j : j + 1])
+        def take_rstd(grp):
             var = work.tile([P, GROUP], F32)
-            nc.gpsimd.tensor_scalar(out=var[:], in0=sum_sq[:], scalar1=1.0 / D_K, scalar2=EPS, op0=ALU.mult, op1=ALU.add)
+            nc.gpsimd.tensor_scalar(out=var[:], in0=square_of[grp][:], scalar1=1.0 / D_K, scalar2=EPS, op0=ALU.mult, op1=ALU.add)
             rstd = work.tile([P, GROUP], F32)
             nc.gpsimd.tensor_tensor(out=rstd[:], in0=var[:], in1=neg_half[:], op=ALU.pow)
             rstd_of[grp] = rstd
 
-        def scale_and_store(grp):
-            o_sb = work.tile([P, GROUP * D_K], F32)
-            for j in range(GROUP):
-                nc.vector.scalar_tensor_tensor(
-                    out=o_sb[:, D_K * j : D_K * (j + 1)].rearrange("p (m e) -> p m e", e=2),
-                    in0=cent_of[(grp, j)][:].rearrange("p (e m) -> p m e", e=2),
-                    scalar=rstd_of[grp][:, j : j + 1],
-                    in1=gamma_bf[:].rearrange("p (m e) -> p m e", e=2),
-                    op0=ALU.mult,
-                    op1=ALU.mult,
-                )
+        def scale(n):
+            grp, j = n // GROUP, n % GROUP
+            if j == 0:
+                o_sb = work.tile([P, GROUP * D_K], F32)
+                o_of[grp] = o_sb
+            nc.vector.scalar_tensor_tensor(
+                out=o_of[grp][:, D_K * j : D_K * (j + 1)].rearrange("p (m e) -> p m e", e=2),
+                in0=cent_of[n][:].rearrange("p (e m) -> p m e", e=2),
+                scalar=rstd_of[grp][:, j : j + 1],
+                in1=gamma_bf[:].rearrange("p (m e) -> p m e", e=2),
+                op0=ALU.mult,
+                op1=ALU.mult,
+            )
+
+        def store(grp):
             rows = out_view[:, GROUP * grp : GROUP * (grp + 1), :]
-            nc.sync.dma_start(out=rows.rearrange("p j c -> p (j c)"), in_=o_sb[:])
+            nc.sync.dma_start(out=rows.rearrange("p j c -> p (j c)"), in_=o_of[grp][:])
 
-        def live(grp):
-            return 0 <= grp < GROUPS
+        def live(n):
+            return 0 <= n < TILES
 
-        for j in range(GROUP):
-            transpose_tile(0, j)
         big_ps = ps_k.tile([P, BLOCK, P], BF16, tag="kk")
         for a in range(BLOCK):
             nc.tensor.transpose(out=big_ps[:, a, :], in_=big_t[:, a, :], identity=ident_b[:])
@@ -299,28 +315,31 @@ def tile_attentionalsplatting_pa_t_kernel(tc, updated_track_tokens, tracks, W_k,
             )
         pos_t = const.tile([P, TILES // BLOCK, P], BF16)
         nc.vector.tensor_copy(out=pos_t[:], in_=pos_ps[:])
-        angles(0)
-        quantise(0)
-        for j in range(GROUP):
-            project_tile(0, j)
-        for j in range(GROUP):
-            transpose_tile(1, j)
-        for i in range(GROUPS + 1):
-            if live(i + LOADS_AHEAD):
-                load(i + LOADS_AHEAD)
-            if live(i + 1):
-                angles(i + 1)
-            if live(i + 2):
-                for j in range(GROUP):
-                    transpose_tile(i + 2, j)
-            if live(i):
-                rotate(i)
-            if live(i + 1):
-                quantise(i + 1)
-                for j in range(GROUP):
-                    project_tile(i + 1, j)
-            if live(i):
-                centre(i)
-                deviation(i)
-            if live(i - 1):
-                scale_and_store(i - 1)
+
+        for s in range(-AHEAD_TRANSPOSE, TILES + BEHIND_SCALE):
+            j = s % GROUP
+            next_grp = s // GROUP + 1
+            if j == 0 and s >= 0 and live(s + GROUP * LOADS_AHEAD):
+                load(s // GROUP + LOADS_AHEAD)
+            if j == 0 and live(GROUP * next_grp):
+                angle_matmul(next_grp)
+            if live(s + AHEAD_TRANSPOSE):
+                transpose_tile(s + AHEAD_TRANSPOSE)
+            if live(s + AHEAD_QUANTISE):
+                quantise(s + AHEAD_QUANTISE)
+            if live(s):
+                rotate(s)
+            if live(s + AHEAD_PROJECT):
+                project(s + AHEAD_PROJECT)
+            if j < 3 and live(GROUP * next_grp):
+                sine_step(next_grp, j)
+            if live(s - BEHIND_CENTRE):
+                centre(s - BEHIND_CENTRE)
+                if j == GROUP - 1:
+                    take_rstd((s - BEHIND_CENTRE) // GROUP)
+            if live(s - BEHIND_SCALE):
+                scale(s - BEHIND_SCALE)
+                if (s - BEHIND_SCALE) % GROUP == GROUP - 1:
+                    store((s - BEHIND_SCALE) // GROUP)
+            if j == GROUP - 1 and live(s):
+                take_mean(s // GROUP)

@@ -30,10 +30,12 @@ MAGIC = 1.5 * 2.0**23
 ROWS = 16
 BLOCK = P // ROWS
 LOADS_AHEAD = 4
-AHEAD_TRANSPOSE = 6
-AHEAD_QUANTISE = 5
-AHEAD_PROJECT = 4
+AHEAD_TRANSPOSE = 5
+AHEAD_COPY = 4
+AHEAD_QUANTISE = 3
+AHEAD_PROJECT = 2
 BEHIND_CENTRE = 4
+BEHIND_SQUARE = 5
 BEHIND_SCALE = 10
 
 FLOPS = 2 * TOKENS * D_IN * D_K
@@ -152,6 +154,7 @@ def tile_attentionalsplatting_pa_t_kernel(tc, updated_track_tokens, tracks, W_k,
                 in_=w_grouped[:, 2048 * g : 2048 * (g + 1)],
             )
 
+        xt_of = {}
         grouped_of = {}
         codes_of = {}
         frac_of = {}
@@ -171,10 +174,13 @@ def tile_attentionalsplatting_pa_t_kernel(tc, updated_track_tokens, tracks, W_k,
             xt = ps_t.tile([P, 4, P], F32, tag="t")
             for s4 in range(4):
                 nc.tensor.transpose(out=xt[:, s4, :], in_=x32[:, first + P * s4 : first + P * (s4 + 1)], identity=ident_f[:])
+            xt_of[n] = xt
+
+        def copy_out(n):
             x_grouped = work.tile([P, D_IN], BF16, align_bytes=64)
             nc.scalar.copy(
                 out=x_grouped[:].bitcast(F32).rearrange("q (g t u) -> q g t u", g=PASSES, u=2),
-                in_=xt[:].rearrange("q (g u) t -> q g t u", u=2),
+                in_=xt_of[n][:].rearrange("q (g u) t -> q g t u", u=2),
             )
             grouped_of[n] = x_grouped
 
@@ -267,11 +273,14 @@ def tile_attentionalsplatting_pa_t_kernel(tc, updated_track_tokens, tracks, W_k,
                 op1=ALU.add,
             )
             cent_of[n] = cent
+
+        def square(n):
+            grp, j = n // GROUP, n % GROUP
             if j == 0:
                 sum_sq = work.tile([P, GROUP], F32)
                 square_of[grp] = sum_sq
             squares = deep.tile([P, D_K], F32)
-            nc.scalar.activation(out=squares[:], in_=cent[:], func=ACT.Square, accum_out=square_of[grp][:, j : j + 1])
+            nc.scalar.activation(out=squares[:], in_=cent_of[n][:], func=ACT.Square, accum_out=square_of[grp][:, j : j + 1])
 
         def take_rstd(grp):
             var = work.tile([P, GROUP], F32)
@@ -325,18 +334,22 @@ def tile_attentionalsplatting_pa_t_kernel(tc, updated_track_tokens, tracks, W_k,
                 angle_matmul(next_grp)
             if live(s + AHEAD_TRANSPOSE):
                 transpose_tile(s + AHEAD_TRANSPOSE)
+            if live(s + AHEAD_COPY):
+                copy_out(s + AHEAD_COPY)
             if live(s + AHEAD_QUANTISE):
                 quantise(s + AHEAD_QUANTISE)
-            if live(s):
-                rotate(s)
             if live(s + AHEAD_PROJECT):
                 project(s + AHEAD_PROJECT)
-            if j < 3 and live(GROUP * next_grp):
-                sine_step(next_grp, j)
+            if live(s):
+                rotate(s)
+            if j > 0 and live(GROUP * next_grp):
+                sine_step(next_grp, j - 1)
             if live(s - BEHIND_CENTRE):
                 centre(s - BEHIND_CENTRE)
-                if j == GROUP - 1:
-                    take_rstd((s - BEHIND_CENTRE) // GROUP)
+            if live(s - BEHIND_SQUARE):
+                square(s - BEHIND_SQUARE)
+                if (s - BEHIND_SQUARE) % GROUP == GROUP - 1:
+                    take_rstd((s - BEHIND_SQUARE) // GROUP)
             if live(s - BEHIND_SCALE):
                 scale(s - BEHIND_SCALE)
                 if (s - BEHIND_SCALE) % GROUP == GROUP - 1:

@@ -36,7 +36,8 @@ AHEAD_QUANTISE = 3
 AHEAD_PROJECT = 2
 BEHIND_CENTRE = 4
 BEHIND_SQUARE = 5
-BEHIND_SCALE = 10
+BEHIND_GAIN = 5
+BEHIND_SCALE = 11
 
 FLOPS = 2 * TOKENS * D_IN * D_K
 
@@ -84,7 +85,7 @@ def tile_attentionalsplatting_pa_t_kernel(tc, updated_track_tokens, tracks, W_k,
         coef = const.tile([P, ROWS // 2], BF16)
         nc.vector.memset(coef[:], 0.0)
         nc.vector.memset(coef[:, 6:8], MAGIC)
-        big_t = const.tile([P, BLOCK, P], BF16)
+        big_t = const.tile([P, BLOCK * (P + ROWS)], BF16)
         nc.vector.memset(big_t[:], 0.0)
         pos = const.tile([P, TILES, ROWS], BF16)
         nc.vector.memset(pos[:], 0.0)
@@ -111,6 +112,8 @@ def tile_attentionalsplatting_pa_t_kernel(tc, updated_track_tokens, tracks, W_k,
         nc.gpsimd.memset(neg_half[:], -0.5)
         gamma_bf = const.tile([P, D_K], BF16)
         nc.gpsimd.dma_start(out=gamma_bf[:], in_=k_gamma.partition_broadcast(P))
+        gamma = const.tile([P, D_K], F32)
+        nc.gpsimd.tensor_scalar(out=gamma[:], in0=gamma_bf[:], scalar1=1.0, scalar2=0.0, op0=ALU.mult, op1=ALU.add)
 
         pieces = const.tile([P, 3], BF16)
         rest1 = const.tile([P, 1], F32)
@@ -122,11 +125,10 @@ def tile_attentionalsplatting_pa_t_kernel(tc, updated_track_tokens, tracks, W_k,
         nc.vector.tensor_copy(out=pieces[:, 2:3], in_=rest2[:])
         for h in range(2):
             nc.vector.tensor_copy(out=coef[FREQS * h : FREQS * (h + 1), 3 * h : 3 * h + 3], in_=pieces[FREQS * h : FREQS * (h + 1), :])
-        for a in range(BLOCK):
-            nc.vector.tensor_copy(
-                out=big_t[:, a, ROWS * a : ROWS * (a + 1)].rearrange("m (s r) -> m s r", s=2),
-                in_=coef[:].unsqueeze(1).to_broadcast([P, 2, ROWS // 2]),
-            )
+        nc.vector.tensor_copy(
+            out=big_t[:].rearrange("m (a c) -> m a c", a=BLOCK)[:, :, 0:ROWS].rearrange("m a (s r) -> m a s r", s=2),
+            in_=coef[:].unsqueeze(1).unsqueeze(1).to_broadcast([P, BLOCK, 2, ROWS // 2]),
+        )
 
         trk_rep = trk[:].rearrange("p (j h) -> p j h", h=2).unsqueeze(3).to_broadcast([P, TILES, 2, 3])
         nc.vector.tensor_copy(out=pos[:, :, 0:6].rearrange("p j (h s) -> p j h s", h=2), in_=trk_rep)
@@ -140,13 +142,13 @@ def tile_attentionalsplatting_pa_t_kernel(tc, updated_track_tokens, tracks, W_k,
         w_grouped5 = w_grouped[:].bitcast(F32).rearrange("q (g l m u) -> q g l m u", g=PASSES, l=PLANES, u=2)
         w_codes = const.tile([P, PASSES, PLANES * P], U32, align_bytes=64)
         w_scales = const.tile([P, PASSES, PLANES * P], U8, align_bytes=64)
-        sources = ((w_sb[:, 0:D_IN], (0, 3)), (w_neg[:], (1,)), (w_sb[:, D_IN : 2 * D_IN], (2,)))
+        sources = ((w_sb[:, 0:D_IN], (0, 3)), (w_sb[:, D_IN : 2 * D_IN], (2,)), (w_neg[:], (1,)))
         for rows, fills in sources:
             wt = ps_t.tile([P, 4, P], F32, tag="t")
             for s in range(4):
                 nc.tensor.transpose(out=wt[:, s, :], in_=rows.bitcast(F32)[:, P * s : P * (s + 1)], identity=ident_f[:])
             for l in fills:
-                nc.vector.tensor_copy(out=w_grouped5[:, :, l, :, :], in_=wt[:].rearrange("q (g u) m -> q g m u", u=2))
+                nc.scalar.copy(out=w_grouped5[:, :, l, :, :], in_=wt[:].rearrange("q (g u) m -> q g m u", u=2))
         for g in range(PASSES):
             nc.vector.quantize_mx(
                 out=w_codes[:, g, :].bitcast(FP8X4),
@@ -289,19 +291,22 @@ def tile_attentionalsplatting_pa_t_kernel(tc, updated_track_tokens, tracks, W_k,
             nc.gpsimd.tensor_tensor(out=rstd[:], in0=var[:], in1=neg_half[:], op=ALU.pow)
             rstd_of[grp] = rstd
 
-        def scale(n):
+        def gain(n):
             grp, j = n // GROUP, n % GROUP
             if j == 0:
                 o_sb = work.tile([P, GROUP * D_K], F32)
                 o_of[grp] = o_sb
-            nc.vector.scalar_tensor_tensor(
+            nc.gpsimd.tensor_tensor(
                 out=o_of[grp][:, D_K * j : D_K * (j + 1)].rearrange("p (m e) -> p m e", e=2),
                 in0=cent_of[n][:].rearrange("p (e m) -> p m e", e=2),
-                scalar=rstd_of[grp][:, j : j + 1],
-                in1=gamma_bf[:].rearrange("p (m e) -> p m e", e=2),
-                op0=ALU.mult,
-                op1=ALU.mult,
+                in1=gamma[:].rearrange("p (m e) -> p m e", e=2),
+                op=ALU.mult,
             )
+
+        def scale(n):
+            grp, j = n // GROUP, n % GROUP
+            rows = o_of[grp][:, D_K * j : D_K * (j + 1)]
+            nc.vector.tensor_scalar(out=rows, in0=rows, scalar1=rstd_of[grp][:, j : j + 1], scalar2=None, op0=ALU.mult)
 
         def store(grp):
             rows = out_view[:, GROUP * grp : GROUP * (grp + 1), :]
@@ -312,9 +317,9 @@ def tile_attentionalsplatting_pa_t_kernel(tc, updated_track_tokens, tracks, W_k,
 
         big_ps = ps_k.tile([P, BLOCK, P], BF16, tag="kk")
         for a in range(BLOCK):
-            nc.tensor.transpose(out=big_ps[:, a, :], in_=big_t[:, a, :], identity=ident_b[:])
+            nc.tensor.transpose(out=big_ps[:, a, :], in_=big_t[:, P * a : P * (a + 1)], identity=ident_b[:])
         big = const.tile([P, BLOCK, P], BF16)
-        nc.vector.tensor_copy(out=big[:], in_=big_ps[:])
+        nc.scalar.copy(out=big[:], in_=big_ps[:])
         pos_ps = ps_k.tile([P, TILES // BLOCK, P], BF16, tag="kk")
         for b in range(TILES // BLOCK):
             nc.tensor.transpose(
@@ -323,7 +328,7 @@ def tile_attentionalsplatting_pa_t_kernel(tc, updated_track_tokens, tracks, W_k,
                 identity=ident_b[:],
             )
         pos_t = const.tile([P, TILES // BLOCK, P], BF16)
-        nc.vector.tensor_copy(out=pos_t[:], in_=pos_ps[:])
+        nc.scalar.copy(out=pos_t[:], in_=pos_ps[:])
 
         for s in range(-AHEAD_TRANSPOSE, TILES + BEHIND_SCALE):
             j = s % GROUP
@@ -346,6 +351,8 @@ def tile_attentionalsplatting_pa_t_kernel(tc, updated_track_tokens, tracks, W_k,
                 sine_step(next_grp, j - 1)
             if live(s - BEHIND_CENTRE):
                 centre(s - BEHIND_CENTRE)
+            if live(s - BEHIND_GAIN):
+                gain(s - BEHIND_GAIN)
             if live(s - BEHIND_SQUARE):
                 square(s - BEHIND_SQUARE)
                 if (s - BEHIND_SQUARE) % GROUP == GROUP - 1:

@@ -36,8 +36,7 @@ AHEAD_QUANTISE = 3
 AHEAD_PROJECT = 2
 BEHIND_CENTRE = 4
 BEHIND_SQUARE = 5
-BEHIND_GAIN = 5
-BEHIND_SCALE = 11
+BEHIND_SCALE = 10
 
 FLOPS = 2 * TOKENS * D_IN * D_K
 
@@ -77,11 +76,29 @@ def tile_attentionalsplatting_pa_t_kernel(tc, updated_track_tokens, tracks, W_k,
         for grp in range(LOADS_AHEAD):
             load(grp)
 
-        ident_f = const.tile([P, P], F32)
-        nc.vector.memset(ident_f[:], 0.0)
-        make_identity(nc, ident_f[:], nomemset=True)
+        idx_i = const.tile([P, 1], I32)
+        for h in range(2):
+            nc.gpsimd.iota(idx_i[FREQS * h : FREQS * (h + 1), :], pattern=[[1, 1]], base=0, channel_multiplier=1)
+        hundred = const.tile([P, 1], F32)
+        nc.vector.memset(hundred[:], 100.0)
         ident_b = const.tile([P, P], BF16)
         nc.vector.memset(ident_b[:], 0.0)
+        ident_f = const.tile([P, P], F32)
+        nc.vector.memset(ident_f[:], 0.0)
+        expo = const.tile([P, 1], F32)
+        nc.vector.tensor_scalar(
+            out=expo[:], in0=idx_i[:], scalar1=-1.0 / FREQS, scalar2=-math.log(2.0 * math.pi) / math.log(100.0),
+            op0=ALU.mult, op1=ALU.add,
+        )
+        turns = const.tile([P, 1], F32)
+        nc.gpsimd.tensor_tensor(out=turns[:], in0=hundred[:], in1=expo[:], op=ALU.pow)
+        make_identity(nc, ident_b[:], nomemset=True)
+        make_identity(nc, ident_f[:], nomemset=True)
+        neg_half = const.tile([P, GROUP], F32)
+        nc.gpsimd.memset(neg_half[:], -0.5)
+        gamma_bf = const.tile([P, D_K], BF16)
+        nc.gpsimd.dma_start(out=gamma_bf[:], in_=k_gamma.partition_broadcast(P))
+
         coef = const.tile([P, ROWS // 2], BF16)
         nc.vector.memset(coef[:], 0.0)
         nc.vector.memset(coef[:, 6:8], MAGIC)
@@ -95,25 +112,6 @@ def tile_attentionalsplatting_pa_t_kernel(tc, updated_track_tokens, tracks, W_k,
         nc.vector.memset(zero[:], 0.0)
         half_pi = const.tile([P, 1], F32)
         nc.vector.tensor_scalar(out=half_pi[:], in0=zero[:], scalar1=math.pi / 2.0, scalar2=None, op0=ALU.add)
-        idx_i = const.tile([P, 1], I32)
-        for h in range(2):
-            nc.gpsimd.iota(idx_i[FREQS * h : FREQS * (h + 1), :], pattern=[[1, 1]], base=0, channel_multiplier=1)
-        hundred = const.tile([P, 1], F32)
-        nc.gpsimd.memset(hundred[:], 100.0)
-        expo = const.tile([P, 1], F32)
-        nc.vector.tensor_scalar(
-            out=expo[:], in0=idx_i[:], scalar1=-1.0 / FREQS, scalar2=-math.log(2.0 * math.pi) / math.log(100.0),
-            op0=ALU.mult, op1=ALU.add,
-        )
-        turns = const.tile([P, 1], F32)
-        nc.gpsimd.tensor_tensor(out=turns[:], in0=hundred[:], in1=expo[:], op=ALU.pow)
-        make_identity(nc, ident_b[:], nomemset=True)
-        neg_half = const.tile([P, GROUP], F32)
-        nc.gpsimd.memset(neg_half[:], -0.5)
-        gamma_bf = const.tile([P, D_K], BF16)
-        nc.gpsimd.dma_start(out=gamma_bf[:], in_=k_gamma.partition_broadcast(P))
-        gamma = const.tile([P, D_K], F32)
-        nc.gpsimd.tensor_scalar(out=gamma[:], in0=gamma_bf[:], scalar1=1.0, scalar2=0.0, op0=ALU.mult, op1=ALU.add)
 
         pieces = const.tile([P, 3], BF16)
         rest1 = const.tile([P, 1], F32)
@@ -129,32 +127,44 @@ def tile_attentionalsplatting_pa_t_kernel(tc, updated_track_tokens, tracks, W_k,
             out=big_t[:].rearrange("m (a c) -> m a c", a=BLOCK)[:, :, 0:ROWS].rearrange("m a (s r) -> m a s r", s=2),
             in_=coef[:].unsqueeze(1).unsqueeze(1).to_broadcast([P, BLOCK, 2, ROWS // 2]),
         )
+        big_ps = ps_k.tile([P, BLOCK, P], BF16, tag="kk")
+        for a in range(BLOCK):
+            nc.tensor.transpose(out=big_ps[:, a, :], in_=big_t[:, P * a : P * (a + 1)], identity=ident_b[:])
+        big = const.tile([P, BLOCK, P], BF16)
+        nc.scalar.copy(out=big[:], in_=big_ps[:])
 
         trk_rep = trk[:].rearrange("p (j h) -> p j h", h=2).unsqueeze(3).to_broadcast([P, TILES, 2, 3])
         nc.vector.tensor_copy(out=pos[:, :, 0:6].rearrange("p j (h s) -> p j h s", h=2), in_=trk_rep)
         nc.vector.tensor_scalar(
             out=pos[:, :, 8:14].rearrange("p j (h s) -> p j h s", h=2), in0=trk_rep, scalar1=-1.0, scalar2=None, op0=ALU.mult
         )
+        pos_ps = ps_k.tile([P, TILES // BLOCK, P], BF16, tag="kk")
+        for b in range(TILES // BLOCK):
+            nc.tensor.transpose(
+                out=pos_ps[:, b, :],
+                in_=pos[:, BLOCK * b : BLOCK * (b + 1), :].rearrange("p j r -> p (j r)"),
+                identity=ident_b[:],
+            )
+        pos_t = const.tile([P, TILES // BLOCK, P], BF16)
+        nc.scalar.copy(out=pos_t[:], in_=pos_ps[:])
 
         w_neg = const.tile([P, D_IN], BF16)
         nc.vector.tensor_scalar(out=w_neg[:], in0=w_sb[:, D_IN : 2 * D_IN], scalar1=-1.0, scalar2=None, op0=ALU.mult)
-        w_grouped = const.tile([P, PASSES * PLANES * P * 4], BF16, align_bytes=64)
-        w_grouped5 = w_grouped[:].bitcast(F32).rearrange("q (g l m u) -> q g l m u", g=PASSES, l=PLANES, u=2)
-        w_codes = const.tile([P, PASSES, PLANES * P], U32, align_bytes=64)
-        w_scales = const.tile([P, PASSES, PLANES * P], U8, align_bytes=64)
+        w_grouped = const.tile([P, PASSES, PLANES, P * 4], BF16, align_bytes=64)
+        w_codes = const.tile([P, PASSES, PLANES, P], U32, align_bytes=64)
+        w_scales = const.tile([P, PASSES, PLANES, P], U8, align_bytes=64)
         sources = ((w_sb[:, 0:D_IN], (0, 3)), (w_sb[:, D_IN : 2 * D_IN], (2,)), (w_neg[:], (1,)))
         for rows, fills in sources:
             wt = ps_t.tile([P, 4, P], F32, tag="t")
             for s in range(4):
                 nc.tensor.transpose(out=wt[:, s, :], in_=rows.bitcast(F32)[:, P * s : P * (s + 1)], identity=ident_f[:])
             for l in fills:
-                nc.scalar.copy(out=w_grouped5[:, :, l, :, :], in_=wt[:].rearrange("q (g u) m -> q g m u", u=2))
-        for g in range(PASSES):
-            nc.vector.quantize_mx(
-                out=w_codes[:, g, :].bitcast(FP8X4),
-                scales=w_scales[:, g, :],
-                in_=w_grouped[:, 2048 * g : 2048 * (g + 1)],
-            )
+                nc.vector.tensor_copy(
+                    out=w_grouped[:, :, l, :].bitcast(F32).rearrange("q g (m u) -> q g m u", u=2),
+                    in_=wt[:].rearrange("q (g u) m -> q g m u", u=2),
+                )
+                for g in range(PASSES):
+                    nc.vector.quantize_mx(out=w_codes[:, g, l, :].bitcast(FP8X4), scales=w_scales[:, g, l, :], in_=w_grouped[:, g, l, :])
 
         xt_of = {}
         grouped_of = {}
@@ -233,8 +243,8 @@ def tile_attentionalsplatting_pa_t_kernel(tc, updated_track_tokens, tracks, W_k,
                     out=kk[:],
                     lhsT=x_codes[:, P * g : P * (g + 1)].bitcast(FP8X4),
                     lhsT_scale=x_scales[:, P * g : P * (g + 1)],
-                    rhs=w_codes[:, g, :].bitcast(FP8X4),
-                    rhs_scale=w_scales[:, g, :],
+                    rhs=w_codes[:, g, :, :].rearrange("q l m -> q (l m)").bitcast(FP8X4),
+                    rhs_scale=w_scales[:, g, :, :].rearrange("q l m -> q (l m)"),
                     start=(g == 0),
                     stop=(g == PASSES - 1),
                 )
@@ -259,7 +269,7 @@ def tile_attentionalsplatting_pa_t_kernel(tc, updated_track_tokens, tracks, W_k,
 
         def take_mean(grp):
             mean = work.tile([P, GROUP], F32)
-            nc.vector.tensor_scalar(out=mean[:], in0=sum_of[grp][:], scalar1=1.0 / D_K, scalar2=None, op0=ALU.mult)
+            nc.scalar.mul(out=mean[:], in_=sum_of[grp][:], mul=1.0 / D_K)
             mean_of[grp] = mean
 
         def centre(n):
@@ -291,44 +301,28 @@ def tile_attentionalsplatting_pa_t_kernel(tc, updated_track_tokens, tracks, W_k,
             nc.gpsimd.tensor_tensor(out=rstd[:], in0=var[:], in1=neg_half[:], op=ALU.pow)
             rstd_of[grp] = rstd
 
-        def gain(n):
+        def scale(n):
             grp, j = n // GROUP, n % GROUP
             if j == 0:
                 o_sb = work.tile([P, GROUP * D_K], F32)
                 o_of[grp] = o_sb
-            nc.gpsimd.tensor_tensor(
+            nc.vector.scalar_tensor_tensor(
                 out=o_of[grp][:, D_K * j : D_K * (j + 1)].rearrange("p (m e) -> p m e", e=2),
                 in0=cent_of[n][:].rearrange("p (e m) -> p m e", e=2),
-                in1=gamma[:].rearrange("p (m e) -> p m e", e=2),
-                op=ALU.mult,
+                scalar=rstd_of[grp][:, j : j + 1],
+                in1=gamma_bf[:].rearrange("p (m e) -> p m e", e=2),
+                op0=ALU.mult,
+                op1=ALU.mult,
             )
 
-        def scale(n):
-            grp, j = n // GROUP, n % GROUP
-            rows = o_of[grp][:, D_K * j : D_K * (j + 1)]
-            nc.vector.tensor_scalar(out=rows, in0=rows, scalar1=rstd_of[grp][:, j : j + 1], scalar2=None, op0=ALU.mult)
-
-        def store(grp):
-            rows = out_view[:, GROUP * grp : GROUP * (grp + 1), :]
-            nc.sync.dma_start(out=rows.rearrange("p j c -> p (j c)"), in_=o_of[grp][:])
+        def store_pair(n):
+            first = D_K * ((n - 1) % GROUP)
+            nc.sync.dma_start(
+                out=out_view[:, n - 1 : n + 1, :].rearrange("p j c -> p (j c)"), in_=o_of[n // GROUP][:, first : first + 2 * D_K]
+            )
 
         def live(n):
             return 0 <= n < TILES
-
-        big_ps = ps_k.tile([P, BLOCK, P], BF16, tag="kk")
-        for a in range(BLOCK):
-            nc.tensor.transpose(out=big_ps[:, a, :], in_=big_t[:, P * a : P * (a + 1)], identity=ident_b[:])
-        big = const.tile([P, BLOCK, P], BF16)
-        nc.scalar.copy(out=big[:], in_=big_ps[:])
-        pos_ps = ps_k.tile([P, TILES // BLOCK, P], BF16, tag="kk")
-        for b in range(TILES // BLOCK):
-            nc.tensor.transpose(
-                out=pos_ps[:, b, :],
-                in_=pos[:, BLOCK * b : BLOCK * (b + 1), :].rearrange("p j r -> p (j r)"),
-                identity=ident_b[:],
-            )
-        pos_t = const.tile([P, TILES // BLOCK, P], BF16)
-        nc.scalar.copy(out=pos_t[:], in_=pos_ps[:])
 
         for s in range(-AHEAD_TRANSPOSE, TILES + BEHIND_SCALE):
             j = s % GROUP
@@ -339,6 +333,8 @@ def tile_attentionalsplatting_pa_t_kernel(tc, updated_track_tokens, tracks, W_k,
                 angle_matmul(next_grp)
             if live(s + AHEAD_TRANSPOSE):
                 transpose_tile(s + AHEAD_TRANSPOSE)
+            if j > 0 and live(GROUP * next_grp):
+                sine_step(next_grp, j - 1)
             if live(s + AHEAD_COPY):
                 copy_out(s + AHEAD_COPY)
             if live(s + AHEAD_QUANTISE):
@@ -347,19 +343,15 @@ def tile_attentionalsplatting_pa_t_kernel(tc, updated_track_tokens, tracks, W_k,
                 project(s + AHEAD_PROJECT)
             if live(s):
                 rotate(s)
-            if j > 0 and live(GROUP * next_grp):
-                sine_step(next_grp, j - 1)
             if live(s - BEHIND_CENTRE):
                 centre(s - BEHIND_CENTRE)
-            if live(s - BEHIND_GAIN):
-                gain(s - BEHIND_GAIN)
             if live(s - BEHIND_SQUARE):
                 square(s - BEHIND_SQUARE)
                 if (s - BEHIND_SQUARE) % GROUP == GROUP - 1:
                     take_rstd((s - BEHIND_SQUARE) // GROUP)
             if live(s - BEHIND_SCALE):
                 scale(s - BEHIND_SCALE)
-                if (s - BEHIND_SCALE) % GROUP == GROUP - 1:
-                    store((s - BEHIND_SCALE) // GROUP)
+                if (s - BEHIND_SCALE) % 2 == 1:
+                    store_pair(s - BEHIND_SCALE)
             if j == GROUP - 1 and live(s):
                 take_mean(s // GROUP)

@@ -26,7 +26,6 @@ GROUP = 4
 GROUPS = TILES // GROUP
 PLANES = 4
 EPS = 1e-6
-MAGIC = 1.5 * 2.0**23
 ROWS = 16
 BLOCK = P // ROWS
 LOADS_AHEAD = 4
@@ -101,13 +100,10 @@ def tile_attentionalsplatting_pa_t_kernel(tc, updated_track_tokens, tracks, W_k,
 
         coef = const.tile([P, ROWS // 2], BF16)
         nc.vector.memset(coef[:], 0.0)
-        nc.vector.memset(coef[:, 6:8], MAGIC)
         big_t = const.tile([P, BLOCK * (P + ROWS)], BF16)
         nc.vector.memset(big_t[:], 0.0)
         pos = const.tile([P, TILES, ROWS], BF16)
         nc.vector.memset(pos[:], 0.0)
-        nc.vector.memset(pos[:, :, 6:7], 1.0)
-        nc.vector.memset(pos[:, :, 7:8], -1.0)
         zero = const.tile([P, 1], F32)
         nc.vector.memset(zero[:], 0.0)
         half_pi = const.tile([P, 1], F32)
@@ -135,9 +131,6 @@ def tile_attentionalsplatting_pa_t_kernel(tc, updated_track_tokens, tracks, W_k,
 
         trk_rep = trk[:].rearrange("p (j h) -> p j h", h=2).unsqueeze(3).to_broadcast([P, TILES, 2, 3])
         nc.vector.tensor_copy(out=pos[:, :, 0:6].rearrange("p j (h s) -> p j h s", h=2), in_=trk_rep)
-        nc.vector.tensor_scalar(
-            out=pos[:, :, 8:14].rearrange("p j (h s) -> p j h s", h=2), in0=trk_rep, scalar1=-1.0, scalar2=None, op0=ALU.mult
-        )
         pos_ps = ps_k.tile([P, TILES // BLOCK, P], BF16, tag="kk")
         for b in range(TILES // BLOCK):
             nc.tensor.transpose(
@@ -169,6 +162,8 @@ def tile_attentionalsplatting_pa_t_kernel(tc, updated_track_tokens, tracks, W_k,
         xt_of = {}
         grouped_of = {}
         codes_of = {}
+        turned_of = {}
+        whole_of = {}
         frac_of = {}
         table_of = {}
         kk_of = {}
@@ -203,15 +198,25 @@ def tile_attentionalsplatting_pa_t_kernel(tc, updated_track_tokens, tracks, W_k,
             codes_of[n] = (x_codes, x_scales)
 
         def angle_matmul(grp):
-            frac = ps_f.tile([P, GROUP * PAIRS], F32)
+            turned = ps_f.tile([P, GROUP * PAIRS], F32)
             a0 = (GROUP * grp) % BLOCK
             nc.tensor.matmul(
-                out=frac[:],
+                out=turned[:],
                 lhsT=pos_t[:, (GROUP * grp) // BLOCK, :],
                 rhs=big[:, a0 : a0 + GROUP, :].rearrange("k a m -> k (a m)"),
                 start=True,
                 stop=True,
             )
+            turned_of[grp] = turned
+
+        def round_turns(grp):
+            whole = work.tile([P, GROUP * PAIRS], I32)
+            nc.vector.tensor_copy(out=whole[:], in_=turned_of[grp][:])
+            whole_of[grp] = whole
+
+        def take_frac(grp):
+            frac = work.tile([P, GROUP * PAIRS], F32)
+            nc.vector.tensor_tensor(out=frac[:], in0=whole_of[grp][:], in1=turned_of[grp][:], op=ALU.subtract)
             frac_abs = work.tile([P, GROUP * PAIRS], F32)
             table = work.tile([P, GROUP * 2 * PAIRS], F32)
             frac_of[grp] = (frac, frac_abs)
@@ -329,8 +334,10 @@ def tile_attentionalsplatting_pa_t_kernel(tc, updated_track_tokens, tracks, W_k,
             next_grp = s // GROUP + 1
             if j == 0 and s >= 0 and live(s + GROUP * LOADS_AHEAD):
                 load(s // GROUP + LOADS_AHEAD)
+            if j == GROUP - 1 and live(GROUP * (next_grp + 1)):
+                angle_matmul(next_grp + 1)
             if j == 0 and live(GROUP * next_grp):
-                angle_matmul(next_grp)
+                round_turns(next_grp)
             if live(s + AHEAD_TRANSPOSE):
                 transpose_tile(s + AHEAD_TRANSPOSE)
             if j > 0 and live(GROUP * next_grp):
@@ -343,6 +350,8 @@ def tile_attentionalsplatting_pa_t_kernel(tc, updated_track_tokens, tracks, W_k,
                 project(s + AHEAD_PROJECT)
             if live(s):
                 rotate(s)
+            if j == 0 and live(GROUP * next_grp):
+                take_frac(next_grp)
             if live(s - BEHIND_CENTRE):
                 centre(s - BEHIND_CENTRE)
             if live(s - BEHIND_SQUARE):

@@ -24,15 +24,17 @@ WORDS = D_IN // 2
 TILES = TOKENS // P
 GROUP = 4
 GROUPS = TILES // GROUP
-PLANES = 4
+PLANES = 3
 EPS = 1e-6
+MAGIC = 1.5 * 2.0**23
 ROWS = 16
+PIECES = 6
 BLOCK = P // ROWS
 LOADS_AHEAD = 4
-AHEAD_TRANSPOSE = 5
-AHEAD_COPY = 4
-AHEAD_QUANTISE = 3
-AHEAD_PROJECT = 2
+AHEAD_TRANSPOSE = 4
+AHEAD_COPY = 3
+AHEAD_QUANTISE = 2
+AHEAD_PROJECT = 1
 BEHIND_CENTRE = 4
 BEHIND_SQUARE = 5
 BEHIND_SCALE = 10
@@ -58,32 +60,39 @@ def tile_attentionalsplatting_pa_t_kernel(tc, updated_track_tokens, tracks, W_k,
 
         x_of = {}
 
-        def load(grp):
+        def load(grp, chunks=(2, 2)):
             x_sb = loads.tile([P, GROUP * D_IN], BF16)
-            for c in range(2):
-                first = GROUP * grp + 2 * c
+            first = 0
+            for tiles in chunks:
                 nc.sync.dma_start(
-                    out=x_sb[:, 2 * D_IN * c : 2 * D_IN * (c + 1)],
-                    in_=x_view[:, first : first + 2, :].rearrange("p j d -> p (j d)"),
+                    out=x_sb[:, D_IN * first : D_IN * (first + tiles)],
+                    in_=x_view[:, GROUP * grp + first : GROUP * grp + first + tiles, :].rearrange("p j d -> p (j d)"),
                 )
+                first += tiles
             x_of[grp] = x_sb
 
         trk = const.tile([P, 2 * TILES], BF16)
-        nc.sync.dma_start(out=trk[:], in_=trk_view)
+        nc.scalar.dma_start(out=trk[:], in_=trk_view)
         w_sb = const.tile([P, 2 * D_IN], BF16)
         nc.sync.dma_start(out=w_sb[:], in_=W_k.rearrange("(m e) k -> m (e k)", e=2))
-        for grp in range(LOADS_AHEAD):
+        load(0, (1, 1, 2))
+        load(1)
+        gamma_bf = const.tile([P, D_K], BF16)
+        nc.sync.dma_start(out=gamma_bf[:], in_=k_gamma.partition_broadcast(P))
+        for grp in range(2, LOADS_AHEAD):
             load(grp)
 
         idx_i = const.tile([P, 1], I32)
         for h in range(2):
             nc.gpsimd.iota(idx_i[FREQS * h : FREQS * (h + 1), :], pattern=[[1, 1]], base=0, channel_multiplier=1)
+        zero = const.tile([P, 1], F32)
+        nc.vector.memset(zero[:], 0.0)
+        warm = const.tile([P, 1], F32)
+        nc.scalar.activation(out=warm[:], in_=zero[:], func=ACT.Sin)
         hundred = const.tile([P, 1], F32)
         nc.vector.memset(hundred[:], 100.0)
         ident_b = const.tile([P, P], BF16)
-        nc.vector.memset(ident_b[:], 0.0)
-        ident_f = const.tile([P, P], F32)
-        nc.vector.memset(ident_f[:], 0.0)
+        nc.vector.memset(ident_b[:].bitcast(I32), 0)
         expo = const.tile([P, 1], F32)
         nc.vector.tensor_scalar(
             out=expo[:], in0=idx_i[:], scalar1=-1.0 / FREQS, scalar2=-math.log(2.0 * math.pi) / math.log(100.0),
@@ -92,20 +101,19 @@ def tile_attentionalsplatting_pa_t_kernel(tc, updated_track_tokens, tracks, W_k,
         turns = const.tile([P, 1], F32)
         nc.gpsimd.tensor_tensor(out=turns[:], in0=hundred[:], in1=expo[:], op=ALU.pow)
         make_identity(nc, ident_b[:], nomemset=True)
-        make_identity(nc, ident_f[:], nomemset=True)
         neg_half = const.tile([P, GROUP], F32)
         nc.gpsimd.memset(neg_half[:], -0.5)
-        gamma_bf = const.tile([P, D_K], BF16)
-        nc.gpsimd.dma_start(out=gamma_bf[:], in_=k_gamma.partition_broadcast(P))
 
-        coef = const.tile([P, ROWS // 2], BF16)
-        nc.vector.memset(coef[:], 0.0)
         big_t = const.tile([P, BLOCK * (P + ROWS)], BF16)
-        nc.vector.memset(big_t[:], 0.0)
+        nc.vector.memset(big_t[:].bitcast(I32), 0)
         pos = const.tile([P, TILES, ROWS], BF16)
-        nc.vector.memset(pos[:], 0.0)
-        zero = const.tile([P, 1], F32)
-        nc.vector.memset(zero[:], 0.0)
+        nc.vector.memset(pos[:].rearrange("p j r -> p (j r)").bitcast(I32), 0)
+        half_of = const.tile([P, 2], BF16)
+        nc.vector.memset(half_of[:], 0.0)
+        for h in range(2):
+            nc.vector.memset(half_of[FREQS * h : FREQS * (h + 1), h : h + 1], 1.0)
+        magic = const.tile([P, 1], F32)
+        nc.vector.memset(magic[:], MAGIC)
         half_pi = const.tile([P, 1], F32)
         nc.vector.tensor_scalar(out=half_pi[:], in0=zero[:], scalar1=math.pi / 2.0, scalar2=None, op0=ALU.add)
 
@@ -117,54 +125,62 @@ def tile_attentionalsplatting_pa_t_kernel(tc, updated_track_tokens, tracks, W_k,
         nc.vector.tensor_copy(out=pieces[:, 1:2], in_=rest1[:])
         nc.vector.tensor_tensor(out=rest2[:], in0=rest1[:], in1=pieces[:, 1:2], op=ALU.subtract)
         nc.vector.tensor_copy(out=pieces[:, 2:3], in_=rest2[:])
-        for h in range(2):
-            nc.vector.tensor_copy(out=coef[FREQS * h : FREQS * (h + 1), 3 * h : 3 * h + 3], in_=pieces[FREQS * h : FREQS * (h + 1), :])
-        nc.vector.tensor_copy(
-            out=big_t[:].rearrange("m (a c) -> m a c", a=BLOCK)[:, :, 0:ROWS].rearrange("m a (s r) -> m a s r", s=2),
-            in_=coef[:].unsqueeze(1).unsqueeze(1).to_broadcast([P, BLOCK, 2, ROWS // 2]),
+        nc.vector.tensor_tensor(
+            out=big_t[:].rearrange("m (a c) -> m a c", a=BLOCK)[:, :, 0:PIECES].rearrange("m a (h s) -> m a h s", h=2),
+            in0=pieces[:].unsqueeze(1).unsqueeze(1).to_broadcast([P, BLOCK, 2, 3]),
+            in1=half_of[:].unsqueeze(1).unsqueeze(3).to_broadcast([P, BLOCK, 2, 3]),
+            op=ALU.mult,
         )
-        big_ps = ps_k.tile([P, BLOCK, P], BF16, tag="kk")
-        for a in range(BLOCK):
-            nc.tensor.transpose(out=big_ps[:, a, :], in_=big_t[:, P * a : P * (a + 1)], identity=ident_b[:])
-        big = const.tile([P, BLOCK, P], BF16)
-        nc.scalar.copy(out=big[:], in_=big_ps[:])
-
         trk_rep = trk[:].rearrange("p (j h) -> p j h", h=2).unsqueeze(3).to_broadcast([P, TILES, 2, 3])
-        nc.vector.tensor_copy(out=pos[:, :, 0:6].rearrange("p j (h s) -> p j h s", h=2), in_=trk_rep)
-        pos_ps = ps_k.tile([P, TILES // BLOCK, P], BF16, tag="kk")
-        for b in range(TILES // BLOCK):
-            nc.tensor.transpose(
-                out=pos_ps[:, b, :],
-                in_=pos[:, BLOCK * b : BLOCK * (b + 1), :].rearrange("p j r -> p (j r)"),
-                identity=ident_b[:],
-            )
+        pos_out = pos[:, :, 0:PIECES].rearrange("p j (h s) -> p j h s", h=2)
+        nc.vector.tensor_copy(out=pos_out[:, 0:BLOCK], in_=trk_rep[:, 0:BLOCK])
+        big = const.tile([P, BLOCK, P], BF16)
         pos_t = const.tile([P, TILES // BLOCK, P], BF16)
-        nc.scalar.copy(out=pos_t[:], in_=pos_ps[:])
 
-        w_neg = const.tile([P, D_IN], BF16)
-        nc.vector.tensor_scalar(out=w_neg[:], in0=w_sb[:, D_IN : 2 * D_IN], scalar1=-1.0, scalar2=None, op0=ALU.mult)
+        def turn_blocks(big_blocks, pos_blocks, copy):
+            n_big = len(big_blocks)
+            both = ps_k.tile([P, BLOCK, P], BF16, tag="kk")
+            for i, a in enumerate(big_blocks):
+                nc.tensor.transpose(out=both[:, i, :], in_=big_t[:, P * a : P * (a + 1)], identity=ident_b[:])
+            for i, b in enumerate(pos_blocks):
+                nc.tensor.transpose(
+                    out=both[:, n_big + i, :],
+                    in_=pos[:, BLOCK * b : BLOCK * (b + 1), :].rearrange("p j r -> p (j r)"),
+                    identity=ident_b[:],
+                )
+            if big_blocks:
+                copy(out=big[:, big_blocks[0] : big_blocks[-1] + 1, :], in_=both[:, 0:n_big, :])
+            copy(out=pos_t[:, pos_blocks[0] : pos_blocks[-1] + 1, :], in_=both[:, n_big : n_big + len(pos_blocks), :])
+
+        turn_blocks((0, 1, 2, 3), (0,), nc.scalar.copy)
+        ident_f = const.tile([P, P], F32)
+        nc.vector.tensor_copy(out=ident_f[:], in_=ident_b[:])
+
         w_grouped = const.tile([P, PASSES, PLANES, P * 4], BF16, align_bytes=64)
         w_codes = const.tile([P, PASSES, PLANES, P], U32, align_bytes=64)
         w_scales = const.tile([P, PASSES, PLANES, P], U8, align_bytes=64)
-        sources = ((w_sb[:, 0:D_IN], (0, 3)), (w_sb[:, D_IN : 2 * D_IN], (2,)), (w_neg[:], (1,)))
-        for rows, fills in sources:
+
+        def turn_w(plane, row, copy):
             wt = ps_t.tile([P, 4, P], F32, tag="t")
             for s in range(4):
-                nc.tensor.transpose(out=wt[:, s, :], in_=rows.bitcast(F32)[:, P * s : P * (s + 1)], identity=ident_f[:])
-            for l in fills:
-                nc.vector.tensor_copy(
-                    out=w_grouped[:, :, l, :].bitcast(F32).rearrange("q g (m u) -> q g m u", u=2),
-                    in_=wt[:].rearrange("q (g u) m -> q g m u", u=2),
-                )
-                for g in range(PASSES):
-                    nc.vector.quantize_mx(out=w_codes[:, g, l, :].bitcast(FP8X4), scales=w_scales[:, g, l, :], in_=w_grouped[:, g, l, :])
+                first = WORDS * row + P * s
+                nc.tensor.transpose(out=wt[:, s, :], in_=w_sb[:].bitcast(F32)[:, first : first + P], identity=ident_f[:])
+            copy(
+                out=w_grouped[:, :, plane, :].bitcast(F32).rearrange("q g (m u) -> q g m u", u=2),
+                in_=wt[:].rearrange("q (g u) m -> q g m u", u=2),
+            )
+
+        def quantise_w(g, first, last):
+            nc.vector.quantize_mx(
+                out=w_codes[:, g, first:last, :].rearrange("q l m -> q (l m)").bitcast(FP8X4),
+                scales=w_scales[:, g, first:last, :].rearrange("q l m -> q (l m)"),
+                in_=w_grouped[:, g, first:last, :].rearrange("q l m -> q (l m)"),
+            )
 
         xt_of = {}
         grouped_of = {}
         codes_of = {}
-        turned_of = {}
-        whole_of = {}
-        frac_of = {}
+        angles_of = {}
         table_of = {}
         kk_of = {}
         prod_of = {}
@@ -207,34 +223,39 @@ def tile_attentionalsplatting_pa_t_kernel(tc, updated_track_tokens, tracks, W_k,
                 start=True,
                 stop=True,
             )
-            turned_of[grp] = turned
-
-        def round_turns(grp):
-            whole = work.tile([P, GROUP * PAIRS], I32)
-            nc.vector.tensor_copy(out=whole[:], in_=turned_of[grp][:])
-            whole_of[grp] = whole
-
-        def take_frac(grp):
+            whole = work.tile([P, GROUP * PAIRS], F32)
             frac = work.tile([P, GROUP * PAIRS], F32)
-            nc.vector.tensor_tensor(out=frac[:], in0=whole_of[grp][:], in1=turned_of[grp][:], op=ALU.subtract)
             frac_abs = work.tile([P, GROUP * PAIRS], F32)
             table = work.tile([P, GROUP * 2 * PAIRS], F32)
-            frac_of[grp] = (frac, frac_abs)
+            angles_of[grp] = (turned, whole, frac, frac_abs)
             table_of[grp] = table
 
-        def sine_step(grp, step):
-            frac, frac_abs = frac_of[grp]
-            table4 = table_of[grp][:].rearrange("p (j r m) -> p j r m", j=GROUP, r=2)
+        def round_turns(grp, first=0, last=GROUP):
+            turned, whole, frac, frac_abs = angles_of[grp]
+            cols = slice(PAIRS * first, PAIRS * last)
+            nc.scalar.activation(out=whole[:, cols], in_=turned[:, cols], func=ACT.Identity, bias=magic[:])
+
+        def take_frac(grp, first=0, last=GROUP):
+            turned, whole, frac, frac_abs = angles_of[grp]
+            cols = slice(PAIRS * first, PAIRS * last)
+            nc.vector.scalar_tensor_tensor(
+                out=frac[:, cols], in0=whole[:, cols], scalar=MAGIC, in1=turned[:, cols], op0=ALU.subtract, op1=ALU.subtract
+            )
+
+        def sine_step(grp, step, first=0, last=GROUP):
+            turned, whole, frac, frac_abs = angles_of[grp]
+            cols = slice(PAIRS * first, PAIRS * last)
+            table4 = table_of[grp][:].rearrange("p (j r m) -> p j r m", j=GROUP, r=2)[:, first:last]
             if step == 0:
-                nc.scalar.activation(out=frac_abs[:], in_=frac[:], func=ACT.Abs)
+                nc.scalar.activation(out=frac_abs[:, cols], in_=frac[:, cols], func=ACT.Abs)
             elif step == 1:
                 nc.scalar.activation(
-                    out=table4[:, :, 1, :], in_=frac[:].rearrange("p (j m) -> p j m", j=GROUP), func=ACT.Sin, scale=-2.0 * math.pi
+                    out=table4[:, :, 1, :], in_=frac[:, cols].rearrange("p (j m) -> p j m", m=PAIRS), func=ACT.Sin, scale=-2.0 * math.pi
                 )
             else:
                 nc.scalar.activation(
                     out=table4[:, :, 0, :],
-                    in_=frac_abs[:].rearrange("p (j m) -> p j m", j=GROUP),
+                    in_=frac_abs[:, cols].rearrange("p (j m) -> p j m", m=PAIRS),
                     func=ACT.Sin,
                     scale=-2.0 * math.pi,
                     bias=half_pi[:],
@@ -242,17 +263,18 @@ def tile_attentionalsplatting_pa_t_kernel(tc, updated_track_tokens, tracks, W_k,
 
         def project(n):
             x_codes, x_scales = codes_of[n]
-            kk = ps_k.tile([P, PLANES * P], F32, tag="kk")
-            for g in range(PASSES):
-                nc.tensor.matmul_mx(
-                    out=kk[:],
-                    lhsT=x_codes[:, P * g : P * (g + 1)].bitcast(FP8X4),
-                    lhsT_scale=x_scales[:, P * g : P * (g + 1)],
-                    rhs=w_codes[:, g, :, :].rearrange("q l m -> q (l m)").bitcast(FP8X4),
-                    rhs_scale=w_scales[:, g, :, :].rearrange("q l m -> q (l m)"),
-                    start=(g == 0),
-                    stop=(g == PASSES - 1),
-                )
+            kk = ps_k.tile([P, 2 * D_K], F32, tag="kk")
+            for d, plane in enumerate((1, 0)):
+                for g in range(PASSES):
+                    nc.tensor.matmul_mx(
+                        out=kk[:, D_K * d : D_K * (d + 1)],
+                        lhsT=x_codes[:, P * g : P * (g + 1)].bitcast(FP8X4),
+                        lhsT_scale=x_scales[:, P * g : P * (g + 1)],
+                        rhs=w_codes[:, g, plane : plane + 2, :].rearrange("q l m -> q (l m)").bitcast(FP8X4),
+                        rhs_scale=w_scales[:, g, plane : plane + 2, :].rearrange("q l m -> q (l m)"),
+                        start=(g == 0),
+                        stop=(g == PASSES - 1),
+                    )
             kk_of[n] = kk
 
         def rotate(n):
@@ -260,7 +282,7 @@ def tile_attentionalsplatting_pa_t_kernel(tc, updated_track_tokens, tracks, W_k,
             if j == 0:
                 sum_r = work.tile([P, GROUP], F32)
                 sum_of[grp] = sum_r
-            prod = deep.tile([P, PLANES * P], F32)
+            prod = deep.tile([P, 2 * D_K], F32)
             nc.vector.scalar_tensor_tensor(
                 out=prod[:].rearrange("p (d x) -> p d x", d=2),
                 in0=kk_of[n][:].rearrange("p (d x) -> p d x", d=2),
@@ -329,27 +351,62 @@ def tile_attentionalsplatting_pa_t_kernel(tc, updated_track_tokens, tracks, W_k,
         def live(n):
             return 0 <= n < TILES
 
-        for s in range(-AHEAD_TRANSPOSE, TILES + BEHIND_SCALE):
+        angle_matmul(0)
+        turn_w(0, 1, nc.vector.tensor_copy)
+        round_turns(0, 0, 1)
+        turn_w(1, 0, nc.scalar.copy)
+        take_frac(0, 0, 1)
+        transpose_tile(0)
+        for g in range(PASSES):
+            quantise_w(g, 0, 2)
+        nc.vector.tensor_scalar(
+            out=w_grouped[:, :, 2, :], in0=w_grouped[:, :, 0, :], scalar1=-1.0, scalar2=None, op0=ALU.mult
+        )
+        for step in range(3):
+            sine_step(0, step, 0, 1)
+        copy_out(0)
+        nc.vector.tensor_copy(out=pos_out[:, BLOCK:], in_=trk_rep[:, BLOCK:])
+        for g in range(PASSES):
+            quantise_w(g, 2, 3)
+        quantise(0)
+        transpose_tile(1)
+        round_turns(0, 1, GROUP)
+        turn_blocks((4, 5, 6, 7), (1, 2, 3), nc.vector.tensor_copy)
+        project(0)
+        copy_out(1)
+        take_frac(0, 1, GROUP)
+        transpose_tile(2)
+        quantise(1)
+        for step in range(3):
+            sine_step(0, step, 1, GROUP)
+        copy_out(2)
+        transpose_tile(3)
+        angle_matmul(1)
+        round_turns(1)
+
+        for s in range(TILES + BEHIND_SCALE):
             j = s % GROUP
             next_grp = s // GROUP + 1
-            if j == 0 and s >= 0 and live(s + GROUP * LOADS_AHEAD):
+            if j == 0 and live(s + GROUP * LOADS_AHEAD):
                 load(s // GROUP + LOADS_AHEAD)
-            if j == GROUP - 1 and live(GROUP * (next_grp + 1)):
+            if j == GROUP - 2 and live(GROUP * (next_grp + 1)):
                 angle_matmul(next_grp + 1)
-            if j == 0 and live(GROUP * next_grp):
-                round_turns(next_grp)
+            if j == GROUP - 1 and live(GROUP * (next_grp + 1)):
+                round_turns(next_grp + 1)
             if live(s + AHEAD_TRANSPOSE):
                 transpose_tile(s + AHEAD_TRANSPOSE)
+            if s == 1:
+                turn_blocks((), (4, 5, 6, 7), nc.scalar.copy)
             if j > 0 and live(GROUP * next_grp):
                 sine_step(next_grp, j - 1)
             if live(s + AHEAD_COPY):
                 copy_out(s + AHEAD_COPY)
+            if live(s):
+                rotate(s)
             if live(s + AHEAD_QUANTISE):
                 quantise(s + AHEAD_QUANTISE)
             if live(s + AHEAD_PROJECT):
                 project(s + AHEAD_PROJECT)
-            if live(s):
-                rotate(s)
             if j == 0 and live(GROUP * next_grp):
                 take_frac(next_grp)
             if live(s - BEHIND_CENTRE):

@@ -37,7 +37,7 @@ AHEAD_QUANTISE = 2
 AHEAD_PROJECT = 1
 BEHIND_CENTRE = 4
 BEHIND_SQUARE = 5
-BEHIND_SCALE = 10
+BEHIND_SCALE = 13
 
 FLOPS = 2 * TOKENS * D_IN * D_K
 
@@ -54,6 +54,7 @@ def tile_attentionalsplatting_pa_t_kernel(tc, updated_track_tokens, tracks, W_k,
         loads = ctx.enter_context(tc.tile_pool(name="loads", bufs=LOADS_AHEAD + 1))
         work = ctx.enter_context(tc.tile_pool(name="work", bufs=3))
         deep = ctx.enter_context(tc.tile_pool(name="deep", bufs=2 * GROUP))
+        cents = ctx.enter_context(tc.tile_pool(name="cents", bufs=BEHIND_SCALE + GROUP + 1))
         ps_t = ctx.enter_context(tc.psum_pool(name="ps_t", bufs=3))
         ps_k = ctx.enter_context(tc.psum_pool(name="ps_k", bufs=GROUP))
         ps_f = ctx.enter_context(tc.psum_pool(name="ps_f", bufs=1))
@@ -152,9 +153,10 @@ def tile_attentionalsplatting_pa_t_kernel(tc, updated_track_tokens, tracks, W_k,
                 copy(out=big[:, big_blocks[0] : big_blocks[-1] + 1, :], in_=both[:, 0:n_big, :])
             copy(out=pos_t[:, pos_blocks[0] : pos_blocks[-1] + 1, :], in_=both[:, n_big : n_big + len(pos_blocks), :])
 
-        turn_blocks((0, 1, 2, 3), (0,), nc.scalar.copy)
+        turn_blocks((0, 1, 2, 3), (0,), nc.vector.tensor_copy)
         ident_f = const.tile([P, P], F32)
         nc.vector.tensor_copy(out=ident_f[:], in_=ident_b[:])
+        nc.vector.tensor_copy(out=pos_out[:, BLOCK:], in_=trk_rep[:, BLOCK:])
 
         w_grouped = const.tile([P, PASSES, PLANES, P * 4], BF16, align_bytes=64)
         w_codes = const.tile([P, PASSES, PLANES, P], U32, align_bytes=64)
@@ -199,9 +201,9 @@ def tile_attentionalsplatting_pa_t_kernel(tc, updated_track_tokens, tracks, W_k,
                 nc.tensor.transpose(out=xt[:, s4, :], in_=x32[:, first + P * s4 : first + P * (s4 + 1)], identity=ident_f[:])
             xt_of[n] = xt
 
-        def copy_out(n):
+        def copy_out(n, copy=nc.scalar.copy):
             x_grouped = work.tile([P, D_IN], BF16, align_bytes=64)
-            nc.scalar.copy(
+            copy(
                 out=x_grouped[:].bitcast(F32).rearrange("q (g t u) -> q g t u", g=PASSES, u=2),
                 in_=xt_of[n][:].rearrange("q (g u) t -> q g t u", u=2),
             )
@@ -302,7 +304,7 @@ def tile_attentionalsplatting_pa_t_kernel(tc, updated_track_tokens, tracks, W_k,
         def centre(n):
             grp, j = n // GROUP, n % GROUP
             prod4 = prod_of[n][:].rearrange("p (e t m) -> p e t m", e=2, t=2)
-            cent = deep.tile([P, D_K], F32)
+            cent = cents.tile([P, D_K], F32)
             nc.vector.scalar_tensor_tensor(
                 out=cent[:].rearrange("p (e m) -> p e m", e=2),
                 in0=prod4[:, :, 0, :],
@@ -351,40 +353,39 @@ def tile_attentionalsplatting_pa_t_kernel(tc, updated_track_tokens, tracks, W_k,
         def live(n):
             return 0 <= n < TILES
 
-        angle_matmul(0)
         turn_w(0, 1, nc.vector.tensor_copy)
-        round_turns(0, 0, 1)
         turn_w(1, 0, nc.scalar.copy)
-        take_frac(0, 0, 1)
+        angle_matmul(0)
         transpose_tile(0)
-        for g in range(PASSES):
-            quantise_w(g, 0, 2)
         nc.vector.tensor_scalar(
             out=w_grouped[:, :, 2, :], in0=w_grouped[:, :, 0, :], scalar1=-1.0, scalar2=None, op0=ALU.mult
         )
-        for step in range(3):
-            sine_step(0, step, 0, 1)
-        copy_out(0)
-        nc.vector.tensor_copy(out=pos_out[:, BLOCK:], in_=trk_rep[:, BLOCK:])
         for g in range(PASSES):
             quantise_w(g, 2, 3)
+        round_turns(0, 0, 1)
+        copy_out(0)
+        take_frac(0, 0, 1)
+        for g in range(PASSES):
+            quantise_w(g, 0, 2)
         quantise(0)
         transpose_tile(1)
-        round_turns(0, 1, GROUP)
         turn_blocks((4, 5, 6, 7), (1, 2, 3), nc.vector.tensor_copy)
-        project(0)
+        for step in range(3):
+            sine_step(0, step, 0, 1)
+        round_turns(0, 1, GROUP)
         copy_out(1)
+        project(0)
         take_frac(0, 1, GROUP)
         transpose_tile(2)
         quantise(1)
         for step in range(3):
             sine_step(0, step, 1, GROUP)
-        copy_out(2)
+        copy_out(2, nc.vector.tensor_copy)
         transpose_tile(3)
         angle_matmul(1)
         round_turns(1)
 
-        for s in range(TILES + BEHIND_SCALE):
+        for s in range(TILES):
             j = s % GROUP
             next_grp = s // GROUP + 1
             if j == 0 and live(s + GROUP * LOADS_AHEAD):
@@ -415,9 +416,23 @@ def tile_attentionalsplatting_pa_t_kernel(tc, updated_track_tokens, tracks, W_k,
                 square(s - BEHIND_SQUARE)
                 if (s - BEHIND_SQUARE) % GROUP == GROUP - 1:
                     take_rstd((s - BEHIND_SQUARE) // GROUP)
-            if live(s - BEHIND_SCALE):
+            if live(s - BEHIND_SCALE) and s < TILES - GROUP:
                 scale(s - BEHIND_SCALE)
                 if (s - BEHIND_SCALE) % 2 == 1:
                     store_pair(s - BEHIND_SCALE)
-            if j == GROUP - 1 and live(s):
+            if j == GROUP - 1:
                 take_mean(s // GROUP)
+
+        square(TILES - GROUP - 1)
+        take_rstd(GROUPS - 2)
+        left = TILES - GROUP - BEHIND_SCALE
+        scale(left)
+        for n in range(TILES - GROUP, TILES):
+            centre(n)
+            square(n)
+        take_rstd(GROUPS - 1)
+        for n in range(left, TILES):
+            if n > left:
+                scale(n)
+            if n % 2 == 1:
+                store_pair(n)

@@ -31,13 +31,17 @@ ROWS = 16
 PIECES = 6
 BLOCK = P // ROWS
 LOADS_AHEAD = 4
-AHEAD_TRANSPOSE = 4
-AHEAD_COPY = 3
+AHEAD_TRANSPOSE = 5
+AHEAD_COPY = 4
 AHEAD_QUANTISE = 2
+SINGLES = 4
 AHEAD_PROJECT = 1
 BEHIND_CENTRE = 4
 BEHIND_SQUARE = 5
-BEHIND_SCALE = 13
+SHORT = TILES - 2 * GROUP
+BEHIND_CENTRE_SHORT = 2
+BEHIND_SQUARE_SHORT = 3
+BEHIND_SCALE = 10
 
 FLOPS = 2 * TOKENS * D_IN * D_K
 
@@ -52,12 +56,12 @@ def tile_attentionalsplatting_pa_t_kernel(tc, updated_track_tokens, tracks, W_k,
         ctx.enter_context(tc.manual_schedule())
         const = ctx.enter_context(tc.tile_pool(name="const", bufs=1))
         loads = ctx.enter_context(tc.tile_pool(name="loads", bufs=LOADS_AHEAD + 1))
-        work = ctx.enter_context(tc.tile_pool(name="work", bufs=3))
+        work = ctx.enter_context(tc.tile_pool(name="work", bufs=4))
         deep = ctx.enter_context(tc.tile_pool(name="deep", bufs=2 * GROUP))
         cents = ctx.enter_context(tc.tile_pool(name="cents", bufs=BEHIND_SCALE + GROUP + 1))
         ps_t = ctx.enter_context(tc.psum_pool(name="ps_t", bufs=3))
-        ps_k = ctx.enter_context(tc.psum_pool(name="ps_k", bufs=GROUP))
-        ps_f = ctx.enter_context(tc.psum_pool(name="ps_f", bufs=1))
+        ps_k = ctx.enter_context(tc.psum_pool(name="ps_k", bufs=3))
+        ps_f = ctx.enter_context(tc.psum_pool(name="ps_f", bufs=2))
 
         x_of = {}
 
@@ -75,7 +79,8 @@ def tile_attentionalsplatting_pa_t_kernel(tc, updated_track_tokens, tracks, W_k,
         trk = const.tile([P, 2 * TILES], BF16)
         nc.scalar.dma_start(out=trk[:], in_=trk_view)
         w_sb = const.tile([P, 2 * D_IN], BF16)
-        nc.sync.dma_start(out=w_sb[:], in_=W_k.rearrange("(m e) k -> m (e k)", e=2))
+        for e in (1, 0):
+            nc.sync.dma_start(out=w_sb[:, D_IN * e : D_IN * (e + 1)], in_=W_k.rearrange("(m e) k -> m e k", e=2)[:, e, :])
         load(0, (1, 1, 2))
         load(1)
         gamma_bf = const.tile([P, D_K], BF16)
@@ -107,34 +112,38 @@ def tile_attentionalsplatting_pa_t_kernel(tc, updated_track_tokens, tracks, W_k,
 
         big_t = const.tile([P, BLOCK * (P + ROWS)], BF16)
         nc.vector.memset(big_t[:].bitcast(I32), 0)
-        pos = const.tile([P, TILES, ROWS], BF16)
-        nc.vector.memset(pos[:].rearrange("p j r -> p (j r)").bitcast(I32), 0)
         half_of = const.tile([P, 2], BF16)
         nc.vector.memset(half_of[:], 0.0)
         for h in range(2):
             nc.vector.memset(half_of[FREQS * h : FREQS * (h + 1), h : h + 1], 1.0)
-        magic = const.tile([P, 1], F32)
-        nc.vector.memset(magic[:], MAGIC)
-        half_pi = const.tile([P, 1], F32)
-        nc.vector.tensor_scalar(out=half_pi[:], in0=zero[:], scalar1=math.pi / 2.0, scalar2=None, op0=ALU.add)
 
         pieces = const.tile([P, 3], BF16)
-        rest1 = const.tile([P, 1], F32)
-        rest2 = const.tile([P, 1], F32)
         nc.vector.tensor_copy(out=pieces[:, 0:1], in_=turns[:])
-        nc.vector.tensor_tensor(out=rest1[:], in0=turns[:], in1=pieces[:, 0:1], op=ALU.subtract)
-        nc.vector.tensor_copy(out=pieces[:, 1:2], in_=rest1[:])
-        nc.vector.tensor_tensor(out=rest2[:], in0=rest1[:], in1=pieces[:, 1:2], op=ALU.subtract)
-        nc.vector.tensor_copy(out=pieces[:, 2:3], in_=rest2[:])
+        nc.vector.tensor_tensor(out=pieces[:, 1:2], in0=turns[:], in1=pieces[:, 0:1], op=ALU.subtract)
+        nc.vector.scalar_tensor_tensor(
+            out=pieces[:, 2:3], in0=turns[:], scalar=pieces[:, 0:1], in1=pieces[:, 1:2], op0=ALU.subtract, op1=ALU.subtract
+        )
         nc.vector.tensor_tensor(
             out=big_t[:].rearrange("m (a c) -> m a c", a=BLOCK)[:, :, 0:PIECES].rearrange("m a (h s) -> m a h s", h=2),
             in0=pieces[:].unsqueeze(1).unsqueeze(1).to_broadcast([P, BLOCK, 2, 3]),
             in1=half_of[:].unsqueeze(1).unsqueeze(3).to_broadcast([P, BLOCK, 2, 3]),
             op=ALU.mult,
         )
+        pos = const.tile([P, TILES, ROWS], BF16)
+        nc.vector.memset(pos[:].rearrange("p j r -> p (j r)").bitcast(I32), 0)
         trk_rep = trk[:].rearrange("p (j h) -> p j h", h=2).unsqueeze(3).to_broadcast([P, TILES, 2, 3])
         pos_out = pos[:, :, 0:PIECES].rearrange("p j (h s) -> p j h s", h=2)
         nc.vector.tensor_copy(out=pos_out[:, 0:BLOCK], in_=trk_rep[:, 0:BLOCK])
+        ident_f = const.tile([P, P], F32)
+        nc.vector.tensor_copy(out=ident_f[:], in_=ident_b[:])
+        neg_ident = const.tile([P, P], BF16)
+        nc.vector.tensor_scalar(out=neg_ident[:], in0=ident_b[:], scalar1=-1.0, scalar2=None, op0=ALU.mult)
+        magic = const.tile([P, 1], F32)
+        nc.vector.memset(magic[:], MAGIC)
+        neg_magic = const.tile([P, 1], F32)
+        nc.vector.memset(neg_magic[:], -MAGIC)
+        half_pi = const.tile([P, 1], F32)
+        nc.vector.tensor_scalar(out=half_pi[:], in0=zero[:], scalar1=math.pi / 2.0, scalar2=None, op0=ALU.add)
         big = const.tile([P, BLOCK, P], BF16)
         pos_t = const.tile([P, TILES // BLOCK, P], BF16)
 
@@ -154,8 +163,6 @@ def tile_attentionalsplatting_pa_t_kernel(tc, updated_track_tokens, tracks, W_k,
             copy(out=pos_t[:, pos_blocks[0] : pos_blocks[-1] + 1, :], in_=both[:, n_big : n_big + len(pos_blocks), :])
 
         turn_blocks((0, 1, 2, 3), (0,), nc.vector.tensor_copy)
-        ident_f = const.tile([P, P], F32)
-        nc.vector.tensor_copy(out=ident_f[:], in_=ident_b[:])
         nc.vector.tensor_copy(out=pos_out[:, BLOCK:], in_=trk_rep[:, BLOCK:])
 
         w_grouped = const.tile([P, PASSES, PLANES, P * 4], BF16, align_bytes=64)
@@ -181,6 +188,7 @@ def tile_attentionalsplatting_pa_t_kernel(tc, updated_track_tokens, tracks, W_k,
 
         xt_of = {}
         grouped_of = {}
+        pair_of = {}
         codes_of = {}
         angles_of = {}
         table_of = {}
@@ -190,6 +198,7 @@ def tile_attentionalsplatting_pa_t_kernel(tc, updated_track_tokens, tracks, W_k,
         sum_of = {}
         mean_of = {}
         square_of = {}
+        var_of = {}
         rstd_of = {}
         o_of = {}
 
@@ -202,35 +211,64 @@ def tile_attentionalsplatting_pa_t_kernel(tc, updated_track_tokens, tracks, W_k,
             xt_of[n] = xt
 
         def copy_out(n, copy=nc.scalar.copy):
-            x_grouped = work.tile([P, D_IN], BF16, align_bytes=64)
+            if n < SINGLES:
+                x_grouped = work.tile([P, D_IN], BF16, align_bytes=64)
+                grouped_of[n] = x_grouped[:]
+            elif n % 2 == 0:
+                x_pair = work.tile([P, 2 * D_IN], BF16, align_bytes=64)
+                grouped_of[n] = x_pair[:, 0:D_IN]
+                grouped_of[n + 1] = x_pair[:, D_IN : 2 * D_IN]
+                pair_of[n] = x_pair
             copy(
-                out=x_grouped[:].bitcast(F32).rearrange("q (g t u) -> q g t u", g=PASSES, u=2),
+                out=grouped_of[n].bitcast(F32).rearrange("q (g t u) -> q g t u", g=PASSES, u=2),
                 in_=xt_of[n][:].rearrange("q (g u) t -> q g t u", u=2),
             )
-            grouped_of[n] = x_grouped
 
         def quantise(n):
-            x_codes = work.tile([P, PASSES * P], U32, align_bytes=64)
-            x_scales = work.tile([P, PASSES * P], U8, align_bytes=64)
-            nc.vector.quantize_mx(out=x_codes[:].bitcast(FP8X4), scales=x_scales[:], in_=grouped_of[n][:])
-            codes_of[n] = (x_codes, x_scales)
+            if n < SINGLES:
+                x_codes = work.tile([P, PASSES * P], U32, align_bytes=64)
+                x_scales = work.tile([P, PASSES * P], U8, align_bytes=64)
+                nc.vector.quantize_mx(out=x_codes[:].bitcast(FP8X4), scales=x_scales[:], in_=grouped_of[n])
+                codes_of[n] = (x_codes[:], x_scales[:])
+            elif n % 2 == 0:
+                pair_codes = work.tile([P, 2 * PASSES * P], U32, align_bytes=64)
+                pair_scales = work.tile([P, 2 * PASSES * P], U8, align_bytes=64)
+                nc.vector.quantize_mx(out=pair_codes[:].bitcast(FP8X4), scales=pair_scales[:], in_=pair_of[n][:])
+                for i in range(2):
+                    cols = slice(PASSES * P * i, PASSES * P * (i + 1))
+                    codes_of[n + i] = (pair_codes[:, cols], pair_scales[:, cols])
 
-        def angle_matmul(grp):
-            turned = ps_f.tile([P, GROUP * PAIRS], F32)
+        def turn_matmul(grp, out, stop):
             a0 = (GROUP * grp) % BLOCK
             nc.tensor.matmul(
-                out=turned[:],
+                out=out[:],
                 lhsT=pos_t[:, (GROUP * grp) // BLOCK, :],
                 rhs=big[:, a0 : a0 + GROUP, :].rearrange("k a m -> k (a m)"),
                 start=True,
-                stop=True,
+                stop=stop,
             )
+
+        def angle_matmul(grp):
+            turned = ps_f.tile([P, GROUP * PAIRS], F32)
+            turn_matmul(grp, turned, True)
             whole = work.tile([P, GROUP * PAIRS], F32)
             frac = work.tile([P, GROUP * PAIRS], F32)
             frac_abs = work.tile([P, GROUP * PAIRS], F32)
             table = work.tile([P, GROUP * 2 * PAIRS], F32)
             angles_of[grp] = (turned, whole, frac, frac_abs)
             table_of[grp] = table
+
+        def by_tensor(grp):
+            return 1 < grp < GROUPS - 1 and grp % 3 == 1
+
+        def whole_to_bf16(grp):
+            turned, whole, frac, frac_abs = angles_of[grp]
+            n_bf = work.tile([P, GROUP * PAIRS], BF16)
+            nc.scalar.activation(out=n_bf[:], in_=whole[:], func=ACT.Identity, bias=neg_magic[:])
+            again = ps_f.tile([P, GROUP * PAIRS], F32, tag="turned")
+            turn_matmul(grp, again, False)
+            nc.tensor.matmul(out=again[:], lhsT=neg_ident[:], rhs=n_bf[:], start=False, stop=True)
+            angles_of[grp] = (again, whole, again, frac_abs)
 
         def round_turns(grp, first=0, last=GROUP):
             turned, whole, frac, frac_abs = angles_of[grp]
@@ -246,13 +284,14 @@ def tile_attentionalsplatting_pa_t_kernel(tc, updated_track_tokens, tracks, W_k,
 
         def sine_step(grp, step, first=0, last=GROUP):
             turned, whole, frac, frac_abs = angles_of[grp]
+            turn = 2.0 * math.pi if by_tensor(grp) else -2.0 * math.pi
             cols = slice(PAIRS * first, PAIRS * last)
             table4 = table_of[grp][:].rearrange("p (j r m) -> p j r m", j=GROUP, r=2)[:, first:last]
             if step == 0:
                 nc.scalar.activation(out=frac_abs[:, cols], in_=frac[:, cols], func=ACT.Abs)
             elif step == 1:
                 nc.scalar.activation(
-                    out=table4[:, :, 1, :], in_=frac[:, cols].rearrange("p (j m) -> p j m", m=PAIRS), func=ACT.Sin, scale=-2.0 * math.pi
+                    out=table4[:, :, 1, :], in_=frac[:, cols].rearrange("p (j m) -> p j m", m=PAIRS), func=ACT.Sin, scale=turn
                 )
             else:
                 nc.scalar.activation(
@@ -296,10 +335,11 @@ def tile_attentionalsplatting_pa_t_kernel(tc, updated_track_tokens, tracks, W_k,
             )
             prod_of[n] = prod
 
-        def take_mean(grp):
-            mean = work.tile([P, GROUP], F32)
-            nc.scalar.mul(out=mean[:], in_=sum_of[grp][:], mul=1.0 / D_K)
-            mean_of[grp] = mean
+        def take_mean(grp, first=0, last=GROUP):
+            if first == 0:
+                mean = work.tile([P, GROUP], F32)
+                mean_of[grp] = mean
+            nc.scalar.mul(out=mean_of[grp][:, first:last], in_=sum_of[grp][:, first:last], mul=1.0 / D_K)
 
         def centre(n):
             grp, j = n // GROUP, n % GROUP
@@ -323,12 +363,25 @@ def tile_attentionalsplatting_pa_t_kernel(tc, updated_track_tokens, tracks, W_k,
             squares = deep.tile([P, D_K], F32)
             nc.scalar.activation(out=squares[:], in_=cent_of[n][:], func=ACT.Square, accum_out=square_of[grp][:, j : j + 1])
 
-        def take_rstd(grp):
-            var = work.tile([P, GROUP], F32)
-            nc.gpsimd.tensor_scalar(out=var[:], in0=square_of[grp][:], scalar1=1.0 / D_K, scalar2=EPS, op0=ALU.mult, op1=ALU.add)
-            rstd = work.tile([P, GROUP], F32)
-            nc.gpsimd.tensor_tensor(out=rstd[:], in0=var[:], in1=neg_half[:], op=ALU.pow)
-            rstd_of[grp] = rstd
+        def take_rstd(grp, first=0, last=GROUP):
+            if first == 0:
+                var = work.tile([P, GROUP], F32)
+                rstd = work.tile([P, GROUP], F32)
+                var_of[grp] = var
+                rstd_of[grp] = rstd
+            cols = slice(first, last)
+            nc.gpsimd.tensor_scalar(
+                out=var_of[grp][:, cols], in0=square_of[grp][:, cols], scalar1=1.0 / D_K, scalar2=EPS, op0=ALU.mult, op1=ALU.add
+            )
+            nc.gpsimd.tensor_tensor(out=rstd_of[grp][:, cols], in0=var_of[grp][:, cols], in1=neg_half[:, cols], op=ALU.pow)
+
+        def square_and_rstd(n):
+            square(n)
+            grp, j = n // GROUP, n % GROUP
+            if n < SHORT and j == GROUP - 1:
+                take_rstd(grp)
+            if n >= SHORT and j % 2 == 1:
+                take_rstd(grp, j - 1, j + 1)
 
         def scale(n):
             grp, j = n // GROUP, n % GROUP
@@ -383,6 +436,8 @@ def tile_attentionalsplatting_pa_t_kernel(tc, updated_track_tokens, tracks, W_k,
         copy_out(2, nc.vector.tensor_copy)
         transpose_tile(3)
         angle_matmul(1)
+        copy_out(3)
+        transpose_tile(4)
         round_turns(1)
 
         for s in range(TILES):
@@ -390,12 +445,19 @@ def tile_attentionalsplatting_pa_t_kernel(tc, updated_track_tokens, tracks, W_k,
             next_grp = s // GROUP + 1
             if j == 0 and live(s + GROUP * LOADS_AHEAD):
                 load(s // GROUP + LOADS_AHEAD)
-            if j == GROUP - 2 and live(GROUP * (next_grp + 1)):
-                angle_matmul(next_grp + 1)
-            if j == GROUP - 1 and live(GROUP * (next_grp + 1)):
-                round_turns(next_grp + 1)
+            later = next_grp + 1
+            if j == GROUP - 2 and later < GROUPS and not by_tensor(later):
+                angle_matmul(later)
+            if j == GROUP - 1 and later < GROUPS and not by_tensor(later):
+                round_turns(later)
+            if j == GROUP - 1 and by_tensor(later + 1):
+                angle_matmul(later + 1)
+            if j == 0 and by_tensor(later):
+                round_turns(later)
             if live(s + AHEAD_TRANSPOSE):
                 transpose_tile(s + AHEAD_TRANSPOSE)
+            if j == 0 and next_grp < GROUPS and by_tensor(next_grp):
+                whole_to_bf16(next_grp)
             if s == 1:
                 turn_blocks((), (4, 5, 6, 7), nc.scalar.copy)
             if j > 0 and live(GROUP * next_grp):
@@ -404,35 +466,36 @@ def tile_attentionalsplatting_pa_t_kernel(tc, updated_track_tokens, tracks, W_k,
                 copy_out(s + AHEAD_COPY)
             if live(s):
                 rotate(s)
+            if j == 0 and 0 < s and next_grp < GROUPS and not by_tensor(next_grp):
+                take_frac(next_grp)
             if live(s + AHEAD_QUANTISE):
                 quantise(s + AHEAD_QUANTISE)
+            if s == 0:
+                take_frac(1)
             if live(s + AHEAD_PROJECT):
                 project(s + AHEAD_PROJECT)
-            if j == 0 and live(GROUP * next_grp):
-                take_frac(next_grp)
-            if live(s - BEHIND_CENTRE):
+            if 0 <= s - BEHIND_CENTRE < SHORT:
                 centre(s - BEHIND_CENTRE)
-            if live(s - BEHIND_SQUARE):
-                square(s - BEHIND_SQUARE)
-                if (s - BEHIND_SQUARE) % GROUP == GROUP - 1:
-                    take_rstd((s - BEHIND_SQUARE) // GROUP)
-            if live(s - BEHIND_SCALE) and s < TILES - GROUP:
+            if s - BEHIND_CENTRE_SHORT >= SHORT:
+                centre(s - BEHIND_CENTRE_SHORT)
+            if 0 <= s - BEHIND_SQUARE < SHORT:
+                square_and_rstd(s - BEHIND_SQUARE)
+            if s - BEHIND_SQUARE_SHORT >= SHORT:
+                square_and_rstd(s - BEHIND_SQUARE_SHORT)
+            if live(s - BEHIND_SCALE):
                 scale(s - BEHIND_SCALE)
                 if (s - BEHIND_SCALE) % 2 == 1:
                     store_pair(s - BEHIND_SCALE)
-            if j == GROUP - 1:
+            if s < SHORT and j == GROUP - 1:
                 take_mean(s // GROUP)
+            if s >= SHORT:
+                take_mean(s // GROUP, j, j + 1)
 
-        square(TILES - GROUP - 1)
-        take_rstd(GROUPS - 2)
-        left = TILES - GROUP - BEHIND_SCALE
-        scale(left)
-        for n in range(TILES - GROUP, TILES):
-            centre(n)
-            square(n)
-        take_rstd(GROUPS - 1)
-        for n in range(left, TILES):
-            if n > left:
-                scale(n)
+        for n in range(TILES - BEHIND_SQUARE_SHORT, TILES):
+            if n >= TILES - BEHIND_CENTRE_SHORT:
+                centre(n)
+            square_and_rstd(n)
+        for n in range(TILES - BEHIND_SCALE, TILES):
+            scale(n)
             if n % 2 == 1:
                 store_pair(n)

@@ -165,6 +165,10 @@ def tile_attentionalsplatting_pa_t_kernel(tc, updated_track_tokens, tracks, W_k,
         turn_blocks((0, 1, 2, 3), (0,), nc.vector.tensor_copy)
         nc.vector.tensor_copy(out=pos_out[:, BLOCK:], in_=trk_rep[:, BLOCK:])
 
+        turns_wide = const.tile([P, P], F32)
+        turns_row = const.tile([P, P], F32)
+        trk_f = const.tile([P, 2 * TILES], F32)
+
         w_grouped = const.tile([P, PASSES, PLANES, P * 4], BF16, align_bytes=64)
         w_codes = const.tile([P, PASSES, PLANES, P], U32, align_bytes=64)
         w_scales = const.tile([P, PASSES, PLANES, P], U8, align_bytes=64)
@@ -190,6 +194,7 @@ def tile_attentionalsplatting_pa_t_kernel(tc, updated_track_tokens, tracks, W_k,
         grouped_of = {}
         pair_of = {}
         codes_of = {}
+        guess_of = {}
         angles_of = {}
         table_of = {}
         kk_of = {}
@@ -259,16 +264,33 @@ def tile_attentionalsplatting_pa_t_kernel(tc, updated_track_tokens, tracks, W_k,
             table_of[grp] = table
 
         def by_tensor(grp):
-            return 1 < grp < GROUPS - 1 and grp % 3 == 1
+            return grp > 1 and grp % 2 == 1
 
-        def whole_to_bf16(grp):
-            turned, whole, frac, frac_abs = angles_of[grp]
+        def guess_turns(grp, j):
+            if j == 0:
+                guess = work.tile([P, GROUP * PAIRS], F32)
+                guess_of[grp] = guess
+            for h in range(2):
+                first = PAIRS * j + FREQS * h
+                place = 2 * (GROUP * grp + j) + h
+                nc.scalar.activation(
+                    out=guess_of[grp][:, first : first + FREQS],
+                    in_=turns_row[:, 0:FREQS],
+                    func=ACT.Identity,
+                    scale=trk_f[:, place : place + 1],
+                    bias=magic[:],
+                )
+
+        def subtract_whole(grp):
             n_bf = work.tile([P, GROUP * PAIRS], BF16)
-            nc.scalar.activation(out=n_bf[:], in_=whole[:], func=ACT.Identity, bias=neg_magic[:])
-            again = ps_f.tile([P, GROUP * PAIRS], F32, tag="turned")
-            turn_matmul(grp, again, False)
-            nc.tensor.matmul(out=again[:], lhsT=neg_ident[:], rhs=n_bf[:], start=False, stop=True)
-            angles_of[grp] = (again, whole, again, frac_abs)
+            nc.scalar.activation(out=n_bf[:], in_=guess_of[grp][:], func=ACT.Identity, bias=neg_magic[:])
+            turned = ps_f.tile([P, GROUP * PAIRS], F32)
+            turn_matmul(grp, turned, False)
+            nc.tensor.matmul(out=turned[:], lhsT=neg_ident[:], rhs=n_bf[:], start=False, stop=True)
+            frac_abs = work.tile([P, GROUP * PAIRS], F32)
+            table = work.tile([P, GROUP * 2 * PAIRS], F32)
+            angles_of[grp] = (turned, turned, turned, frac_abs)
+            table_of[grp] = table
 
         def round_turns(grp, first=0, last=GROUP):
             turned, whole, frac, frac_abs = angles_of[grp]
@@ -450,14 +472,18 @@ def tile_attentionalsplatting_pa_t_kernel(tc, updated_track_tokens, tracks, W_k,
                 angle_matmul(later)
             if j == GROUP - 1 and later < GROUPS and not by_tensor(later):
                 round_turns(later)
-            if j == GROUP - 1 and by_tensor(later + 1):
-                angle_matmul(later + 1)
-            if j == 0 and by_tensor(later):
-                round_turns(later)
+            if later < GROUPS and by_tensor(later):
+                guess_turns(later, j)
             if live(s + AHEAD_TRANSPOSE):
                 transpose_tile(s + AHEAD_TRANSPOSE)
             if j == 0 and next_grp < GROUPS and by_tensor(next_grp):
-                whole_to_bf16(next_grp)
+                subtract_whole(next_grp)
+            if s == 2:
+                turns_ps = ps_f.tile([P, P], F32, tag="turned")
+                nc.vector.tensor_copy(out=turns_wide[:], in_=turns[:].to_broadcast([P, P]))
+                nc.tensor.transpose(out=turns_ps[:], in_=turns_wide[:], identity=ident_f[:])
+                nc.scalar.copy(out=turns_row[:], in_=turns_ps[:])
+                nc.vector.tensor_copy(out=trk_f[:], in_=trk[:])
             if s == 1:
                 turn_blocks((), (4, 5, 6, 7), nc.scalar.copy)
             if j > 0 and live(GROUP * next_grp):

import math
from contextlib import ExitStack

import concourse.mybir as mybir
from concourse.masks import make_identity

FP8X4 = mybir.dt.float8_e4m3fn_x4
BF16 = mybir.dt.bfloat16
F32 = mybir.dt.float32
I32 = mybir.dt.int32
U32 = mybir.dt.uint32
U8 = mybir.dt.uint8
ALU = mybir.AluOpType
ACT = mybir.ActivationFunctionType

P = 128
TOKENS = 16 * 512
D_IN = 1024
D_K = 256
PAIRS = D_K // 2
FREQS = PAIRS // 2
PASSES = 2
WORDS = D_IN // 2
TILES = TOKENS // P
GROUP = 4
GROUPS = TILES // GROUP
PLANES = 3
EPS = 1e-6
MAGIC = 1.5 * 2.0**23
ROWS = 16
PIECES = 6
BLOCK = P // ROWS
LOADS_AHEAD = 4
AHEAD_TRANSPOSE = 5
AHEAD_COPY = 4
AHEAD_QUANTISE = 2
SINGLES = 4
AHEAD_PROJECT = 1
BEHIND_CENTRE = 4
BEHIND_SQUARE = 5
SHORT = TILES - 2 * GROUP
BEHIND_CENTRE_SHORT = 2
BEHIND_SQUARE_SHORT = 3
BEHIND_SCALE = 10

FLOPS = 2 * TOKENS * D_IN * D_K


def tile_attentionalsplatting_pa_t_kernel(tc, updated_track_tokens, tracks, W_k, k_gamma, out):
    nc = tc.nc
    x_view = updated_track_tokens.rearrange("t (a j) d -> (t a) j d", j=TILES)
    out_view = out.rearrange("t (a j) c -> (t a) j c", j=TILES)
    trk_view = tracks.rearrange("t (a j) h -> (t a) (j h)", j=TILES)

    with ExitStack() as ctx:
        ctx.enter_context(tc.manual_schedule())
        const = ctx.enter_context(tc.tile_pool(name="const", bufs=1))
        loads = ctx.enter_context(tc.tile_pool(name="loads", bufs=LOADS_AHEAD + 1))
        work = ctx.enter_context(tc.tile_pool(name="work", bufs=4))
        deep = ctx.enter_context(tc.tile_pool(name="deep", bufs=2 * GROUP))
        cents = ctx.enter_context(tc.tile_pool(name="cents", bufs=BEHIND_SCALE + GROUP + 1))
        ps_t = ctx.enter_context(tc.psum_pool(name="ps_t", bufs=3))
        ps_k = ctx.enter_context(tc.psum_pool(name="ps_k", bufs=3))
        ps_f = ctx.enter_context(tc.psum_pool(name="ps_f", bufs=2))

        x_of = {}

        def load(grp, chunks=(2, 2)):
            x_sb = loads.tile([P, GROUP * D_IN], BF16)
            first = 0
            for tiles in chunks:
                nc.sync.dma_start(
                    out=x_sb[:, D_IN * first : D_IN * (first + tiles)],
                    in_=x_view[:, GROUP * grp + first : GROUP * grp + first + tiles, :].rearrange("p j d -> p (j d)"),
                )
                first += tiles
            x_of[grp] = x_sb

        trk = const.tile([P, 2 * TILES], BF16)
        nc.scalar.dma_start(out=trk[:], in_=trk_view)
        w_sb = const.tile([P, 2 * D_IN], BF16)
        for e in (1, 0):
            nc.sync.dma_start(out=w_sb[:, D_IN * e : D_IN * (e + 1)], in_=W_k.rearrange("(m e) k -> m e k", e=2)[:, e, :])
        load(0, (1, 1, 2))
        load(1)
        gamma_bf = const.tile([P, D_K], BF16)
        nc.sync.dma_start(out=gamma_bf[:], in_=k_gamma.partition_broadcast(P))
        for grp in range(2, LOADS_AHEAD):
            load(grp)

        idx_i = const.tile([P, 1], I32)
        for h in range(2):
            nc.gpsimd.iota(idx_i[FREQS * h : FREQS * (h + 1), :], pattern=[[1, 1]], base=0, channel_multiplier=1)
        zero = const.tile([P, 1], F32)
        nc.vector.memset(zero[:], 0.0)
        warm = const.tile([P, 1], F32)
        nc.scalar.activation(out=warm[:], in_=zero[:], func=ACT.Sin)
        hundred = const.tile([P, 1], F32)
        nc.vector.memset(hundred[:], 100.0)
        ident_b = const.tile([P, P], BF16)
        nc.vector.memset(ident_b[:].bitcast(I32), 0)
        expo = const.tile([P, 1], F32)
        nc.vector.tensor_scalar(
            out=expo[:], in0=idx_i[:], scalar1=-1.0 / FREQS, scalar2=-math.log(2.0 * math.pi) / math.log(100.0),
            op0=ALU.mult, op1=ALU.add,
        )
        turns = const.tile([P, 1], F32)
        nc.gpsimd.tensor_tensor(out=turns[:], in0=hundred[:], in1=expo[:], op=ALU.pow)
        make_identity(nc, ident_b[:], nomemset=True)
        neg_half = const.tile([P, GROUP], F32)
        nc.gpsimd.memset(neg_half[:], -0.5)

        big_t = const.tile([P, BLOCK * (P + ROWS)], BF16)
        nc.vector.memset(big_t[:].bitcast(I32), 0)
        half_of = const.tile([P, 2], BF16)
        nc.vector.memset(half_of[:], 0.0)
        for h in range(2):
            nc.vector.memset(half_of[FREQS * h : FREQS * (h + 1), h : h + 1], 1.0)

        pieces = const.tile([P, 3], BF16)
        nc.vector.tensor_copy(out=pieces[:, 0:1], in_=turns[:])
        nc.vector.tensor_tensor(out=pieces[:, 1:2], in0=turns[:], in1=pieces[:, 0:1], op=ALU.subtract)
        nc.vector.scalar_tensor_tensor(
            out=pieces[:, 2:3], in0=turns[:], scalar=pieces[:, 0:1], in1=pieces[:, 1:2], op0=ALU.subtract, op1=ALU.subtract
        )
        nc.vector.tensor_tensor(
            out=big_t[:].rearrange("m (a c) -> m a c", a=BLOCK)[:, :, 0:PIECES].rearrange("m a (h s) -> m a h s", h=2),
            in0=pieces[:].unsqueeze(1).unsqueeze(1).to_broadcast([P, BLOCK, 2, 3]),
            in1=half_of[:].unsqueeze(1).unsqueeze(3).to_broadcast([P, BLOCK, 2, 3]),
            op=ALU.mult,
        )
        pos = const.tile([P, TILES, ROWS], BF16)
        nc.vector.memset(pos[:].rearrange("p j r -> p (j r)").bitcast(I32), 0)
        trk_rep = trk[:].rearrange("p (j h) -> p j h", h=2).unsqueeze(3).to_broadcast([P, TILES, 2, 3])
        pos_out = pos[:, :, 0:PIECES].rearrange("p j (h s) -> p j h s", h=2)
        nc.vector.tensor_copy(out=pos_out[:, 0:BLOCK], in_=trk_rep[:, 0:BLOCK])
        ident_f = const.tile([P, P], F32)
        nc.vector.tensor_copy(out=ident_f[:], in_=ident_b[:])
        neg_ident = const.tile([P, P], BF16)
        nc.vector.tensor_scalar(out=neg_ident[:], in0=ident_b[:], scalar1=-1.0, scalar2=None, op0=ALU.mult)
        magic = const.tile([P, 1], F32)
        nc.vector.memset(magic[:], MAGIC)
        neg_magic = const.tile([P, 1], F32)
        nc.vector.memset(neg_magic[:], -MAGIC)
        half_pi = const.tile([P, 1], F32)
        nc.vector.tensor_scalar(out=half_pi[:], in0=zero[:], scalar1=math.pi / 2.0, scalar2=None, op0=ALU.add)
        big = const.tile([P, BLOCK, P], BF16)
        pos_t = const.tile([P, TILES // BLOCK, P], BF16)

        def turn_blocks(big_blocks, pos_blocks, copy):
            n_big = len(big_blocks)
            both = ps_k.tile([P, BLOCK, P], BF16, tag="kk")
            for i, a in enumerate(big_blocks):
                nc.tensor.transpose(out=both[:, i, :], in_=big_t[:, P * a : P * (a + 1)], identity=ident_b[:])
            for i, b in enumerate(pos_blocks):
                nc.tensor.transpose(
                    out=both[:, n_big + i, :],
                    in_=pos[:, BLOCK * b : BLOCK * (b + 1), :].rearrange("p j r -> p (j r)"),
                    identity=ident_b[:],
                )
            if big_blocks:
                copy(out=big[:, big_blocks[0] : big_blocks[-1] + 1, :], in_=both[:, 0:n_big, :])
            copy(out=pos_t[:, pos_blocks[0] : pos_blocks[-1] + 1, :], in_=both[:, n_big : n_big + len(pos_blocks), :])

        turn_blocks((0, 1, 2, 3), (0,), nc.vector.tensor_copy)
        nc.vector.tensor_copy(out=pos_out[:, BLOCK:], in_=trk_rep[:, BLOCK:])

        turns_wide = const.tile([P, P], F32)
        turns_row = const.tile([P, P], F32)
        trk_f = const.tile([P, 2 * TILES], F32)

        w_grouped = const.tile([P, PASSES, PLANES, P * 4], BF16, align_bytes=64)
        w_codes = const.tile([P, PASSES, PLANES, P], U32, align_bytes=64)
        w_scales = const.tile([P, PASSES, PLANES, P], U8, align_bytes=64)

        def turn_w(plane, row, copy):
            wt = ps_t.tile([P, 4, P], F32, tag="t")
            for s in range(4):
                first = WORDS * row + P * s
                nc.tensor.transpose(out=wt[:, s, :], in_=w_sb[:].bitcast(F32)[:, first : first + P], identity=ident_f[:])
            copy(
                out=w_grouped[:, :, plane, :].bitcast(F32).rearrange("q g (m u) -> q g m u", u=2),
                in_=wt[:].rearrange("q (g u) m -> q g m u", u=2),
            )

        def quantise_w(g, first, last):
            nc.vector.quantize_mx(
                out=w_codes[:, g, first:last, :].rearrange("q l m -> q (l m)").bitcast(FP8X4),
                scales=w_scales[:, g, first:last, :].rearrange("q l m -> q (l m)"),
                in_=w_grouped[:, g, first:last, :].rearrange("q l m -> q (l m)"),
            )

        xt_of = {}
        grouped_of = {}
        pair_of = {}
        codes_of = {}
        guess_of = {}
        angles_of = {}
        table_of = {}
        kk_of = {}
        prod_of = {}
        cent_of = {}
        sum_of = {}
        mean_of = {}
        square_of = {}
        var_of = {}
        rstd_of = {}
        o_of = {}

        def transpose_tile(n):
            first = WORDS * (n % GROUP)
            x32 = x_of[n // GROUP][:].bitcast(F32)
            xt = ps_t.tile([P, 4, P], F32, tag="t")
            for s4 in range(4):
                nc.tensor.transpose(out=xt[:, s4, :], in_=x32[:, first + P * s4 : first + P * (s4 + 1)], identity=ident_f[:])
            xt_of[n] = xt

        def copy_out(n, copy=nc.scalar.copy):
            if n < SINGLES:
                x_grouped = work.tile([P, D_IN], BF16, align_bytes=64)
                grouped_of[n] = x_grouped[:]
            elif n % 2 == 0:
                x_pair = work.tile([P, 2 * D_IN], BF16, align_bytes=64)
                grouped_of[n] = x_pair[:, 0:D_IN]
                grouped_of[n + 1] = x_pair[:, D_IN : 2 * D_IN]
                pair_of[n] = x_pair
            copy(
                out=grouped_of[n].bitcast(F32).rearrange("q (g t u) -> q g t u", g=PASSES, u=2),
                in_=xt_of[n][:].rearrange("q (g u) t -> q g t u", u=2),
            )

        def quantise(n):
            if n < SINGLES:
                x_codes = work.tile([P, PASSES * P], U32, align_bytes=64)
                x_scales = work.tile([P, PASSES * P], U8, align_bytes=64)
                nc.vector.quantize_mx(out=x_codes[:].bitcast(FP8X4), scales=x_scales[:], in_=grouped_of[n])
                codes_of[n] = (x_codes[:], x_scales[:])
            elif n % 2 == 0:
                pair_codes = work.tile([P, 2 * PASSES * P], U32, align_bytes=64)
                pair_scales = work.tile([P, 2 * PASSES * P], U8, align_bytes=64)
                nc.vector.quantize_mx(out=pair_codes[:].bitcast(FP8X4), scales=pair_scales[:], in_=pair_of[n][:])
                for i in range(2):
                    cols = slice(PASSES * P * i, PASSES * P * (i + 1))
                    codes_of[n + i] = (pair_codes[:, cols], pair_scales[:, cols])

        def turn_matmul(grp, out, stop):
            a0 = (GROUP * grp) % BLOCK
            nc.tensor.matmul(
                out=out[:],
                lhsT=pos_t[:, (GROUP * grp) // BLOCK, :],
                rhs=big[:, a0 : a0 + GROUP, :].rearrange("k a m -> k (a m)"),
                start=True,
                stop=stop,
            )

        def angle_matmul(grp):
            turned = ps_f.tile([P, GROUP * PAIRS], F32)
            turn_matmul(grp, turned, True)
            whole = work.tile([P, GROUP * PAIRS], F32)
            frac = work.tile([P, GROUP * PAIRS], F32)
            frac_abs = work.tile([P, GROUP * PAIRS], F32)
            table = work.tile([P, GROUP * 2 * PAIRS], F32)
            angles_of[grp] = (turned, whole, frac, frac_abs)
            table_of[grp] = table

        def by_tensor(grp):
            return grp > 1 and grp % 2 == 1

        def guess_turns(grp, j):
            if j == 0:
                guess = work.tile([P, GROUP * PAIRS], F32)
                guess_of[grp] = guess
            for h in range(2):
                first = PAIRS * j + FREQS * h
                place = 2 * (GROUP * grp + j) + h
                nc.scalar.activation(
                    out=guess_of[grp][:, first : first + FREQS],
                    in_=turns_row[:, 0:FREQS],
                    func=ACT.Identity,
                    scale=trk_f[:, place : place + 1],
                    bias=magic[:],
                )

        def subtract_whole(grp):
            n_bf = work.tile([P, GROUP * PAIRS], BF16)
            nc.scalar.activation(out=n_bf[:], in_=guess_of[grp][:], func=ACT.Identity, bias=neg_magic[:])
            turned = ps_f.tile([P, GROUP * PAIRS], F32)
            turn_matmul(grp, turned, False)
            nc.tensor.matmul(out=turned[:], lhsT=neg_ident[:], rhs=n_bf[:], start=False, stop=True)
            frac_abs = work.tile([P, GROUP * PAIRS], F32)
            table = work.tile([P, GROUP * 2 * PAIRS], F32)
            angles_of[grp] = (turned, turned, turned, frac_abs)
            table_of[grp] = table

        def round_turns(grp, first=0, last=GROUP):
            turned, whole, frac, frac_abs = angles_of[grp]
            cols = slice(PAIRS * first, PAIRS * last)
            nc.scalar.activation(out=whole[:, cols], in_=turned[:, cols], func=ACT.Identity, bias=magic[:])

        def take_frac(grp, first=0, last=GROUP):
            turned, whole, frac, frac_abs = angles_of[grp]
            cols = slice(PAIRS * first, PAIRS * last)
            nc.vector.scalar_tensor_tensor(
                out=frac[:, cols], in0=whole[:, cols], scalar=MAGIC, in1=turned[:, cols], op0=ALU.subtract, op1=ALU.subtract
            )

        def sine_step(grp, step, first=0, last=GROUP):
            turned, whole, frac, frac_abs = angles_of[grp]
            turn = 2.0 * math.pi if by_tensor(grp) else -2.0 * math.pi
            cols = slice(PAIRS * first, PAIRS * last)
            table4 = table_of[grp][:].rearrange("p (j r m) -> p j r m", j=GROUP, r=2)[:, first:last]
            if step == 0:
                nc.scalar.activation(out=frac_abs[:, cols], in_=frac[:, cols], func=ACT.Abs)
            elif step == 1:
                nc.scalar.activation(
                    out=table4[:, :, 1, :], in_=frac[:, cols].rearrange("p (j m) -> p j m", m=PAIRS), func=ACT.Sin, scale=turn
                )
            else:
                nc.scalar.activation(
                    out=table4[:, :, 0, :],
                    in_=frac_abs[:, cols].rearrange("p (j m) -> p j m", m=PAIRS),
                    func=ACT.Sin,
                    scale=-2.0 * math.pi,
                    bias=half_pi[:],
                )

        def project(n):
            x_codes, x_scales = codes_of[n]
            kk = ps_k.tile([P, 2 * D_K], F32, tag="kk")
            for d, plane in enumerate((1, 0)):
                for g in range(PASSES):
                    nc.tensor.matmul_mx(
                        out=kk[:, D_K * d : D_K * (d + 1)],
                        lhsT=x_codes[:, P * g : P * (g + 1)].bitcast(FP8X4),
                        lhsT_scale=x_scales[:, P * g : P * (g + 1)],
                        rhs=w_codes[:, g, plane : plane + 2, :].rearrange("q l m -> q (l m)").bitcast(FP8X4),
                        rhs_scale=w_scales[:, g, plane : plane + 2, :].rearrange("q l m -> q (l m)"),
                        start=(g == 0),
                        stop=(g == PASSES - 1),
                    )
            kk_of[n] = kk

        def rotate(n):
            grp, j = n // GROUP, n % GROUP
            if j == 0:
                sum_r = work.tile([P, GROUP], F32)
                sum_of[grp] = sum_r
            prod = deep.tile([P, 2 * D_K], F32)
            nc.vector.scalar_tensor_tensor(
                out=prod[:].rearrange("p (d x) -> p d x", d=2),
                in0=kk_of[n][:].rearrange("p (d x) -> p d x", d=2),
                scalar=1.0,
                in1=table_of[grp][:, D_K * j : D_K * (j + 1)].unsqueeze(1).to_broadcast([P, 2, D_K]),
                op0=ALU.mult,
                op1=ALU.mult,
                accum_out=sum_of[grp][:, j : j + 1],
            )
            prod_of[n] = prod

        def take_mean(grp, first=0, last=GROUP):
            if first == 0:
                mean = work.tile([P, GROUP], F32)
                mean_of[grp] = mean
            nc.scalar.mul(out=mean_of[grp][:, first:last], in_=sum_of[grp][:, first:last], mul=1.0 / D_K)

        def centre(n):
            grp, j = n // GROUP, n % GROUP
            prod4 = prod_of[n][:].rearrange("p (e t m) -> p e t m", e=2, t=2)
            cent = cents.tile([P, D_K], F32)
            nc.vector.scalar_tensor_tensor(
                out=cent[:].rearrange("p (e m) -> p e m", e=2),
                in0=prod4[:, :, 0, :],
                scalar=mean_of[grp][:, j : j + 1],
                in1=prod4[:, :, 1, :],
                op0=ALU.subtract,
                op1=ALU.add,
            )
            cent_of[n] = cent

        def square(n):
            grp, j = n // GROUP, n % GROUP
            if j == 0:
                sum_sq = work.tile([P, GROUP], F32)
                square_of[grp] = sum_sq
            squares = deep.tile([P, D_K], F32)
            nc.scalar.activation(out=squares[:], in_=cent_of[n][:], func=ACT.Square, accum_out=square_of[grp][:, j : j + 1])

        def take_rstd(grp, first=0, last=GROUP):
            if first == 0:
                var = work.tile([P, GROUP], F32)
                rstd = work.tile([P, GROUP], F32)
                var_of[grp] = var
                rstd_of[grp] = rstd
            cols = slice(first, last)
            nc.gpsimd.tensor_scalar(
                out=var_of[grp][:, cols], in0=square_of[grp][:, cols], scalar1=1.0 / D_K, scalar2=EPS, op0=ALU.mult, op1=ALU.add
            )
            nc.gpsimd.tensor_tensor(out=rstd_of[grp][:, cols], in0=var_of[grp][:, cols], in1=neg_half[:, cols], op=ALU.pow)

        def square_and_rstd(n):
            square(n)
            grp, j = n // GROUP, n % GROUP
            if n < SHORT and j == GROUP - 1:
                take_rstd(grp)
            if n >= SHORT and j % 2 == 1:
                take_rstd(grp, j - 1, j + 1)

        def scale(n):
            grp, j = n // GROUP, n % GROUP
            if j == 0:
                o_sb = work.tile([P, GROUP * D_K], F32)
                o_of[grp] = o_sb
            nc.vector.scalar_tensor_tensor(
                out=o_of[grp][:, D_K * j : D_K * (j + 1)].rearrange("p (m e) -> p m e", e=2),
                in0=cent_of[n][:].rearrange("p (e m) -> p m e", e=2),
                scalar=rstd_of[grp][:, j : j + 1],
                in1=gamma_bf[:].rearrange("p (m e) -> p m e", e=2),
                op0=ALU.mult,
                op1=ALU.mult,
            )

        def store_pair(n):
            first = D_K * ((n - 1) % GROUP)
            nc.sync.dma_start(
                out=out_view[:, n - 1 : n + 1, :].rearrange("p j c -> p (j c)"), in_=o_of[n // GROUP][:, first : first + 2 * D_K]
            )

        def live(n):
            return 0 <= n < TILES

        turn_w(0, 1, nc.vector.tensor_copy)
        turn_w(1, 0, nc.scalar.copy)
        angle_matmul(0)
        transpose_tile(0)
        nc.vector.tensor_scalar(
            out=w_grouped[:, :, 2, :], in0=w_grouped[:, :, 0, :], scalar1=-1.0, scalar2=None, op0=ALU.mult
        )
        for g in range(PASSES):
            quantise_w(g, 2, 3)
        round_turns(0, 0, 1)
        copy_out(0)
        take_frac(0, 0, 1)
        for g in range(PASSES):
            quantise_w(g, 0, 2)
        quantise(0)
        transpose_tile(1)
        turn_blocks((4, 5, 6, 7), (1, 2, 3), nc.vector.tensor_copy)
        for step in range(3):
            sine_step(0, step, 0, 1)
        round_turns(0, 1, GROUP)
        copy_out(1)
        project(0)
        take_frac(0, 1, GROUP)
        transpose_tile(2)
        quantise(1)
        for step in range(3):
            sine_step(0, step, 1, GROUP)
        copy_out(2, nc.vector.tensor_copy)
        transpose_tile(3)
        angle_matmul(1)
        copy_out(3)
        transpose_tile(4)
        round_turns(1)

        for s in range(TILES):
            j = s % GROUP
            next_grp = s // GROUP + 1
            if j == 0 and live(s + GROUP * LOADS_AHEAD):
                load(s // GROUP + LOADS_AHEAD)
            later = next_grp + 1
            if j == GROUP - 2 and later < GROUPS and not by_tensor(later):
                angle_matmul(later)
            if j == GROUP - 1 and later < GROUPS and not by_tensor(later):
                round_turns(later)
            if later < GROUPS and by_tensor(later):
                guess_turns(later, j)
            if live(s + AHEAD_TRANSPOSE):
                transpose_tile(s + AHEAD_TRANSPOSE)
            if j == 0 and next_grp < GROUPS and by_tensor(next_grp):
                subtract_whole(next_grp)
            if s == 2:
                turns_ps = ps_f.tile([P, P], F32, tag="turned")
                nc.vector.tensor_copy(out=turns_wide[:], in_=turns[:].to_broadcast([P, P]))
                nc.tensor.transpose(out=turns_ps[:], in_=turns_wide[:], identity=ident_f[:])
                nc.scalar.copy(out=turns_row[:], in_=turns_ps[:])
                nc.vector.tensor_copy(out=trk_f[:], in_=trk[:])
            if s == 1:
                turn_blocks((), (4, 5, 6, 7), nc.scalar.copy)
            if j > 0 and live(GROUP * next_grp):
                sine_step(next_grp, j - 1)
            if live(s + AHEAD_COPY):
                copy_out(s + AHEAD_COPY)
            if live(s):
                rotate(s)
            if j == 0 and 0 < s and next_grp < GROUPS and not by_tensor(next_grp):
                take_frac(next_grp)
            if live(s + AHEAD_QUANTISE):
                quantise(s + AHEAD_QUANTISE)
            if s == 0:
                take_frac(1)
            if live(s + AHEAD_PROJECT):
                project(s + AHEAD_PROJECT)
            if 0 <= s - BEHIND_CENTRE < SHORT:
                centre(s - BEHIND_CENTRE)
            if s - BEHIND_CENTRE_SHORT >= SHORT:
                centre(s - BEHIND_CENTRE_SHORT)
            if 0 <= s - BEHIND_SQUARE < SHORT:
                square_and_rstd(s - BEHIND_SQUARE)
            if s - BEHIND_SQUARE_SHORT >= SHORT:
                square_and_rstd(s - BEHIND_SQUARE_SHORT)
            if live(s - BEHIND_SCALE):
                scale(s - BEHIND_SCALE)
                if (s - BEHIND_SCALE) % 2 == 1:
                    store_pair(s - BEHIND_SCALE)
            if s < SHORT and j == GROUP - 1:
                take_mean(s // GROUP)
            if s >= SHORT:
                take_mean(s // GROUP, j, j + 1)

        for n in range(TILES - BEHIND_SQUARE_SHORT, TILES):
            if n >= TILES - BEHIND_CENTRE_SHORT:
                centre(n)
            square_and_rstd(n)
        for n in range(TILES - BEHIND_SCALE, TILES):
            scale(n)
            if n % 2 == 1:
                store_pair(n)
